import numpy as np
import ml_dtypes


def mxq(x, axis, fmt="e4m3"):
    dtype, down = {"e4m3": (ml_dtypes.float8_e4m3fn, 7), "e5m2": (ml_dtypes.float8_e5m2, 14)}[fmt]
    v = np.moveaxis(np.asarray(x, np.float32).astype(ml_dtypes.bfloat16).astype(np.float64), axis, -1)
    blocks = v.reshape(v.shape[:-1] + (-1, 32))
    amax = np.abs(blocks).max(-1, keepdims=True)
    byte = np.maximum(np.where(amax > 0, np.frexp(amax)[1] - 1 + 127, 0) - down, 1)
    scale = np.exp2(byte - 127.0)
    codes = (blocks / scale).astype(np.float32).astype(dtype).astype(np.float64)
    return np.moveaxis((codes * scale).reshape(v.shape), -1, axis)


WIDE = False


def mx_kscale(k):
    if not WIDE:
        return np.ones(k)
    levels = np.array([10, -10, 5, -5, 0])
    a = np.random.permutation(np.resize(levels, k // 512 * 4)).reshape(k // 512, 4)
    idx = np.arange(k)
    return np.exp2(a[idx // 512, idx % 128 // 32])


BF16 = ml_dtypes.bfloat16


def bf(x):
    return np.asarray(x, np.float32).astype(BF16)


def f64(x):
    return np.asarray(x).astype(np.float64)


BATCH, IN_FEATURES, OUT_FEATURES, LOG_DIM = 512, 2048, 2048, 11
BUTTERFLY_DIM = 2 ** LOG_DIM
MAX_BLOCKS = BUTTERFLY_DIM // 2


def setup_inputs():
    s = mx_kscale(IN_FEATURES)
    x = np.random.standard_normal((BATCH, IN_FEATURES)) * s
    w_in = np.random.standard_normal((BUTTERFLY_DIM, IN_FEATURES)) / np.sqrt(IN_FEATURES) / s[None, :]
    w_out = np.random.standard_normal((OUT_FEATURES, BUTTERFLY_DIM)) / np.sqrt(BUTTERFLY_DIM)
    b_out = np.random.standard_normal(OUT_FEATURES) * 0.1
    theta = np.random.uniform(0.0, 1.0, (LOG_DIM, MAX_BLOCKS))
    return {"x": bf(x), "w_in": bf(w_in), "w_out": bf(w_out), "b_out": bf(b_out),
            "a_pad": bf(np.cos(theta)), "b_pad": bf(np.sin(theta))}


def _butterfly(x, a_pad, b_pad):
    B = x.shape[0]
    for l in range(LOG_DIM):
        block_size = 2 ** l
        num_blocks = BUTTERFLY_DIM // (2 * block_size)
        a = a_pad[l, :num_blocks][None, :, None]
        b = b_pad[l, :num_blocks][None, :, None]
        xv = x.reshape(B, num_blocks, 2, block_size)
        x0 = xv[:, :, 0, :]
        x1 = xv[:, :, 1, :]
        top = a * x0 + b * x1
        bot = -b * x0 + a * x1
        x = np.stack([top, bot], axis=2).reshape(B, BUTTERFLY_DIM)
    return x


def reference(x, w_in, w_out, b_out, a_pad, b_pad):
    h = mxq(f64(x), 1, "e4m3") @ mxq(f64(w_in), 1, "e4m3").T
    h = _butterfly(h, f64(a_pad), f64(b_pad))
    return (mxq(h, 1, "e4m3") @ mxq(f64(w_out), 1, "e4m3").T) + f64(b_out)

@@ -1,0 +1,218 @@
+from contextlib import ExitStack
+
+import concourse.mybir as mybir
+from concourse.masks import make_identity
+
+F32 = mybir.dt.float32
+BF16 = mybir.dt.bfloat16
+U32 = mybir.dt.uint32
+U8 = mybir.dt.uint8
+FP8X4 = mybir.dt.float8_e4m3fn_x4
+ALU = mybir.AluOpType
+ACTF = mybir.ActivationFunctionType
+P = 128
+FLOPS = 2 * 2 * 512 * 2048 * 2048 + 11 * 3 * 512 * 2048
+
+
+def tile_butterflylayer_kernel(tc, x, w_in, w_out, b_out, a_pad, b_pad, out):
+    nc = tc.nc
+    pads = (a_pad, b_pad)
+    with ExitStack() as ctx:
+        const = ctx.enter_context(tc.tile_pool(name="const", bufs=1))
+        rawp = ctx.enter_context(tc.tile_pool(name="rawp", bufs=5))
+        grpp = ctx.enter_context(tc.tile_pool(name="grpp", bufs=3))
+        wqp = ctx.enter_context(tc.tile_pool(name="wqp", bufs=3))
+        k2 = ctx.enter_context(tc.tile_pool(name="k2", bufs=4))
+        k4 = ctx.enter_context(tc.tile_pool(name="k4", bufs=8))
+        tps = ctx.enter_context(tc.psum_pool(name="tps", bufs=3))
+        accp = ctx.enter_context(tc.psum_pool(name="accp", bufs=5))
+
+        identF = const.tile([P, P], F32, name="identF")
+        make_identity(nc, identF[:])
+        ET = const.tile([P, 2 * P], F32, name="ET")
+        nc.gpsimd.memset(ET[:], 1.0)
+        for i in range(7):
+            n = 64 >> i
+            off = P - 2 * n
+            seg = ET[:, 2 * off:2 * off + 2 * n]
+            nc.gpsimd.affine_select(out=seg, in_=seg, pattern=[[-(1 << i), 2 * n]],
+                                    compare_op=ALU.is_ge, fill=0.0, base=0, channel_multiplier=1)
+            nc.gpsimd.affine_select(out=seg, in_=seg, pattern=[[1 << i, 2 * n]],
+                                    compare_op=ALU.is_ge, fill=0.0, base=(1 << i) - 1, channel_multiplier=-1)
+        identB = const.tile([P, P], BF16, name="identB")
+        make_identity(nc, identB[:])
+
+        V0 = const.tile([P, P], BF16, name="V0")
+        nc.vector.memset(V0[:], 0.0)
+        U = const.tile([P, P], BF16, name="U")
+        nc.vector.memset(U[:], 0.0)
+        hcb = const.tile([P, 6, 16], BF16, name="hcb")
+
+        raws = []
+        for gp in range(2):
+            raw = rawp.tile([P, 4096], BF16, name="raw", tag="raw")
+            nc.sync.dma_start(out=raw[:].rearrange("p (t k) -> p t k", t=4),
+                              in_=x[:, 1024 * gp:1024 * gp + 1024].rearrange("(t p) k -> p t k", p=P))
+            raws.append(raw)
+        with nc.allow_non_contiguous_dma(reason="small coefficient tables"):
+            for arr in range(2):
+                nc.scalar.dma_start(out=V0[8 * arr:8 * arr + 8, :],
+                                    in_=pads[arr][0:1, :].rearrange("o (h c) -> (o h) c", c=P))
+            for i in range(7):
+                n = 64 >> i
+                off = P - 2 * n
+                for arr in range(2):
+                    r0 = 56 * arr + 8 * i
+                    nc.scalar.dma_start(out=U[r0:r0 + 8, off:off + n],
+                                        in_=pads[arr][i + 1:i + 2, 0:8 * n].rearrange("o (h q) -> (o h) q", q=n))
+            for arr in range(2):
+                for l in range(3):
+                    nc.gpsimd.dma_start(out=hcb[:, 3 * arr + l, 0:4],
+                                        in_=pads[arr][8 + l:9 + l, 0:4].rearrange("o j -> (o j)").partition_broadcast(P))
+        for h in range(8):
+            raw = rawp.tile([P, 4096], BF16, name="raw", tag="raw")
+            nc.sync.dma_start(out=raw[:], in_=w_in[256 * h:256 * h + 256, :].rearrange("(p e) k -> p (e k)", e=2))
+            raws.append(raw)
+        for oc in range(4):
+            for cp in range(2):
+                raw = rawp.tile([P, 4096], BF16, name="raw", tag="raw")
+                nc.sync.dma_start(out=raw[:].rearrange("p (t k) -> p t k", t=4),
+                                  in_=w_out[512 * oc:512 * oc + 512, 1024 * cp:1024 * cp + 1024].rearrange("(t p) k -> p t k", p=P))
+                raws.append(raw)
+        bias = const.tile([P, 2048], BF16, name="bias")
+        nc.sync.dma_start(out=bias[:], in_=b_out.partition_broadcast(P))
+
+        def prepare(raw, codes, scales, moving, copies):
+            rawW = raw[:].bitcast(F32)
+            grp = grpp.tile([P, 4096], BF16, name="grp", tag="grp", align_bytes=64)
+            grpW = grp[:].bitcast(F32)
+            for a in range(2):
+                for b2 in range(2):
+                    bank = tps.tile([P, 512], F32, name="bank", tag="tp")
+                    for u in range(2):
+                        for s in range(2):
+                            if moving:
+                                src = (2 * b2 + s) * 512 + 256 * a + 128 * u
+                            else:
+                                src = a * 1024 + 256 * (2 * b2 + s) + 128 * u
+                            d = u * 256 + s * 128
+                            nc.tensor.transpose(bank[:, d:d + 128], rawW[:, src:src + 128], identF[:])
+                    dst = (a * 512 + b2 * 256) * 2
+                    copies[2 * a + b2](out=grpW[:, dst:dst + 512].rearrange("p (c u) -> p c u", u=2),
+                                       in_=bank[:].rearrange("p (u c) -> p c u", u=2))
+            nc.vector.quantize_mx(out=codes.bitcast(FP8X4), scales=scales, in_=grp[:])
+
+        sc = nc.scalar.copy
+        vc = nc.vector.tensor_copy
+
+        xq = const.tile([P, 2048], U32, name="xq", align_bytes=64)
+        xs = const.tile([P, 2048], U8, name="xs", align_bytes=64)
+        for gp in range(2):
+            prepare(raws[gp], xq[:, 1024 * gp:1024 * gp + 1024], xs[:, 1024 * gp:1024 * gp + 1024], True, (vc, vc, vc, vc))
+
+        v0ps = tps.tile([P, P], BF16, name="v0ps", tag="tp")
+        nc.tensor.transpose(v0ps[:], V0[:], identB[:])
+        c0 = const.tile([P, 16], F32, name="c0")
+        nc.vector.tensor_copy(out=c0[:], in_=v0ps[:, 0:16])
+
+        ups = tps.tile([P, P], BF16, name="ups", tag="tp")
+        nc.tensor.transpose(ups[:], U[:], identB[:])
+        R = const.tile([P, 2, 56, 2], BF16, name="R")
+        nc.vector.tensor_copy(out=R[:, 0, :, 0], in_=ups[:, 0:56])
+        nc.vector.tensor_scalar_mul(out=R[:, 0, :, 1], in0=ups[:, 56:112], scalar1=-1.0)
+        nc.vector.tensor_copy(out=R[:, 1, :, 0], in_=ups[:, 56:112])
+        nc.vector.tensor_copy(out=R[:, 1, :, 1], in_=ups[:, 0:56])
+
+        eps = tps.tile([P, 2, P], F32, name="eps", tag="tp")
+        for z in range(2):
+            nc.tensor.transpose(eps[:, z, :], ET[:].rearrange("p (c z) -> p z c", z=2)[:, z, :], identF[:])
+        E = const.tile([P, 2, P], BF16, name="E")
+        nc.vector.tensor_copy(out=E[:], in_=eps[:])
+        fps = tps.tile([P, 112], F32, name="fps", tag="tp")
+        for z in range(2):
+            nc.tensor.matmul(out=fps[:], lhsT=E[:, z, :], rhs=R[:, z].rearrange("p r o -> p (r o)"),
+                             start=(z == 0), stop=(z == 1))
+        F = const.tile([P, 7, 8, 2], F32, name="F")
+        nc.vector.tensor_copy(out=F[:].rearrange("p i h o -> p (i h o)"), in_=fps[:])
+        prev = F[:, 0]
+        for i in range(1, 7):
+            r = 1 << i
+            nxt = const.tile([P, 8, 2 * r], F32, name="lt%d" % i)
+            nc.vector.tensor_tensor(out=nxt[:].rearrange("p h (o r) -> p h o r", o=2),
+                                    in0=F[:, i].unsqueeze(3).to_broadcast([P, 8, 2, r]),
+                                    in1=prev.unsqueeze(2).to_broadcast([P, 8, 2, r]), op=ALU.mult)
+            prev = nxt[:]
+        LT = prev
+
+        hc = const.tile([P, 6, 4], F32, name="hc")
+        nc.vector.tensor_copy(out=hc[:], in_=hcb[:, :, 0:4])
+
+        def rotate(x0, x1, ca, cb, o0, o1, pool, shape):
+            t1 = pool.tile(shape, F32, name="t1", tag="t", align_bytes=64)
+            t2 = pool.tile(shape, F32, name="t2", tag="t", align_bytes=64)
+            nc.scalar.activation(out=t1[:], in_=x1, func=ACTF.Copy, scale=cb)
+            nc.scalar.activation(out=t2[:], in_=x0, func=ACTF.Copy, scale=cb)
+            nc.vector.scalar_tensor_tensor(out=o0, in0=x0, scalar=ca, in1=t1[:], op0=ALU.mult, op1=ALU.add)
+            nc.vector.scalar_tensor_tensor(out=o1, in0=x1, scalar=ca, in1=t2[:], op0=ALU.mult, op1=ALU.subtract)
+
+        y = const.tile([P, 16, 512], F32, name="y")
+        s0s = {}
+        for h in range(8):
+            wq = wqp.tile([P, 1024], U32, name="wq", tag="wq", align_bytes=64)
+            ws = wqp.tile([P, 1024], U8, name="ws", tag="ws", align_bytes=64)
+            prepare(raws[2 + h], wq[:], ws[:], False, (sc, sc, sc, sc))
+            accs = []
+            for e in range(2):
+                acc = accp.tile([P, 512], F32, name="acc", tag="acc")
+                for g in range(4):
+                    c = (4 * e + g) * 128
+                    nc.tensor.matmul_mx(out=acc[:], lhsT=wq[:, c:c + 128].bitcast(FP8X4), lhsT_scale=ws[:, c:c + 128],
+                                        rhs=xq[:, 512 * g:512 * g + 512].bitcast(FP8X4), rhs_scale=xs[:, 512 * g:512 * g + 512],
+                                        start=(g == 0), stop=(g == 3))
+                accs.append(acc)
+            s0 = k4.tile([P, 2, 512], F32, name="s0", tag="t", align_bytes=64)
+            rotate(accs[0][:], accs[1][:], c0[:, h:h + 1], c0[:, 8 + h:9 + h], s0[:, 0, :], s0[:, 1, :], k2, [P, 512])
+            s0s[h] = s0
+            if h % 2 == 1:
+                j = h // 2
+                for e in range(2):
+                    lps = []
+                    for hh in (h - 1, h):
+                        lp = accp.tile([P, 512], F32, name="lp", tag="acc")
+                        nc.tensor.matmul(out=lp[:], lhsT=LT[:, hh, :], rhs=s0s[hh][:, e, :], start=True, stop=True)
+                        lps.append(lp)
+                    rotate(lps[0][:], lps[1][:], hc[:, 0, j:j + 1], hc[:, 3, j:j + 1],
+                           y[:, 2 * (h - 1) + e, :], y[:, 2 * h + e, :], k2, [P, 512])
+            if h % 4 == 3:
+                j = h // 4
+                for hl in range(2):
+                    r0 = 8 * j + 2 * hl
+                    rotate(y[:, r0:r0 + 2, :], y[:, r0 + 4:r0 + 6, :], hc[:, 1, j:j + 1], hc[:, 4, j:j + 1],
+                           y[:, r0:r0 + 2, :], y[:, r0 + 4:r0 + 6, :], k4, [P, 2, 512])
+
+        woq = const.tile([P, 8192], U32, name="woq", align_bytes=64)
+        wos = const.tile([P, 8192], U8, name="wos", align_bytes=64)
+        for un in range(8):
+            prepare(raws[10 + un], woq[:, 1024 * un:1024 * un + 1024], wos[:, 1024 * un:1024 * un + 1024], True, (sc, sc, sc, vc))
+
+        for bt in range(4):
+            cols = slice(128 * bt, 128 * bt + 128)
+            gb = k4.tile([P, 16, 128], BF16, name="gb", tag="t", align_bytes=64)
+            rotate(y[:, 0:8, cols], y[:, 8:16, cols], hc[:, 2, 0:1], hc[:, 5, 0:1], gb[:, 0:8, :], gb[:, 8:16, :], k4, [P, 8, 128])
+            gg = k4.tile([P, 4, 128, 4], BF16, name="gg", tag="t", align_bytes=64)
+            nc.vector.tensor_copy(out=gg[:], in_=gb[:].rearrange("p (c t) b -> p c b t", t=4))
+            gq = const.tile([P, 512], U32, name="gq%d" % bt, align_bytes=64)
+            gs = const.tile([P, 512], U8, name="gs%d" % bt, align_bytes=64)
+            nc.vector.quantize_mx(out=gq[:].bitcast(FP8X4), scales=gs[:], in_=gg[:].rearrange("p c b t -> p (c b t)"))
+            for op in range(2):
+                osb = k4.tile([P, 1024], F32, name="osb", tag="t", align_bytes=64)
+                for o2 in range(2):
+                    oc = 2 * op + o2
+                    acc = accp.tile([P, 512], F32, name="acc2", tag="acc")
+                    for c in range(4):
+                        m = (4 * oc + c) * 512
+                        nc.tensor.matmul_mx(out=acc[:], lhsT=gq[:, 128 * c:128 * c + 128].bitcast(FP8X4), lhsT_scale=gs[:, 128 * c:128 * c + 128],
+                                            rhs=woq[:, m:m + 512].bitcast(FP8X4), rhs_scale=wos[:, m:m + 512],
+                                            start=(c == 0), stop=(c == 3))
+                    nc.vector.tensor_tensor(out=osb[:, 512 * o2:512 * o2 + 512], in0=acc[:], in1=bias[:, 512 * oc:512 * oc + 512], op=ALU.add)
+                nc.sync.dma_start(out=out[128 * bt:128 * bt + 128, 1024 * op:1024 * op + 1024], in_=osb[:])

@@ -10,7 +10,9 @@ U8 = mybir.dt.uint8
 FP8X4 = mybir.dt.float8_e4m3fn_x4
 ALU = mybir.AluOpType
 ACTF = mybir.ActivationFunctionType
+AXIS = mybir.AxisListType
 P = 128
+HALF = 256
 FLOPS = 2 * 2 * 512 * 2048 * 2048 + 11 * 3 * 512 * 2048
 
 
@@ -21,198 +23,361 @@ def tile_butterflylayer_kernel(tc, x, w_in, w_out, b_out, a_pad, b_pad, out):
         const = ctx.enter_context(tc.tile_pool(name="const", bufs=1))
         rawp = ctx.enter_context(tc.tile_pool(name="rawp", bufs=5))
         grpp = ctx.enter_context(tc.tile_pool(name="grpp", bufs=3))
-        wqp = ctx.enter_context(tc.tile_pool(name="wqp", bufs=3))
+        wqp = ctx.enter_context(tc.tile_pool(name="wqp", bufs=10))
         k2 = ctx.enter_context(tc.tile_pool(name="k2", bufs=4))
-        k4 = ctx.enter_context(tc.tile_pool(name="k4", bufs=8))
-        tps = ctx.enter_context(tc.psum_pool(name="tps", bufs=3))
-        accp = ctx.enter_context(tc.psum_pool(name="accp", bufs=5))
+        s0p = ctx.enter_context(tc.tile_pool(name="s0p", bufs=6))
+        k4 = ctx.enter_context(tc.tile_pool(name="k4", bufs=4))
+        ggp = ctx.enter_context(tc.tile_pool(name="ggp", bufs=2))
+        gqp = ctx.enter_context(tc.tile_pool(name="gqp", bufs=4))
+        osp = ctx.enter_context(tc.tile_pool(name="osp", bufs=5))
+        tps = ctx.enter_context(tc.psum_pool(name="tps", bufs=4))
+        accp = ctx.enter_context(tc.psum_pool(name="accp", bufs=4))
+
+        sc = nc.scalar.copy
+        vc = nc.vector.tensor_copy
 
         identF = const.tile([P, P], F32, name="identF")
         make_identity(nc, identF[:])
-        ET = const.tile([P, 2 * P], F32, name="ET")
-        nc.gpsimd.memset(ET[:], 1.0)
-        for i in range(7):
-            n = 64 >> i
-            off = P - 2 * n
-            seg = ET[:, 2 * off:2 * off + 2 * n]
-            nc.gpsimd.affine_select(out=seg, in_=seg, pattern=[[-(1 << i), 2 * n]],
-                                    compare_op=ALU.is_ge, fill=0.0, base=0, channel_multiplier=1)
-            nc.gpsimd.affine_select(out=seg, in_=seg, pattern=[[1 << i, 2 * n]],
-                                    compare_op=ALU.is_ge, fill=0.0, base=(1 << i) - 1, channel_multiplier=-1)
-        identB = const.tile([P, P], BF16, name="identB")
-        make_identity(nc, identB[:])
-
         V0 = const.tile([P, P], BF16, name="V0")
         nc.vector.memset(V0[:], 0.0)
         U = const.tile([P, P], BF16, name="U")
         nc.vector.memset(U[:], 0.0)
-        hcb = const.tile([P, 6, 16], BF16, name="hcb")
 
-        raws = []
-        for gp in range(2):
+        raws = {}
+
+        def new_raw(key):
             raw = rawp.tile([P, 4096], BF16, name="raw", tag="raw")
+            raws[key] = raw
+            return raw
+
+        def load_x(half):
+            raw = new_raw(("x", half))
+            for a in range(2):
+                nc.sync.dma_start(out=raw[:].rearrange("p (t k) -> p t k", t=2)[:, :, 1024 * a:1024 * a + 1024],
+                                  in_=x[HALF * half:HALF * half + HALF, 1024 * a:1024 * a + 1024].rearrange("(t p) k -> p t k", p=P))
+
+        def load_in(h):
+            raw = new_raw(h)
+            nc.sync.dma_start(out=raw[:], in_=w_in[256 * h:256 * h + 256, :].rearrange("(p e) k -> p (e k)", e=2))
+
+        def load_out(un):
+            oc, cp = un // 2, un % 2
+            raw = new_raw(8 + un)
             nc.sync.dma_start(out=raw[:].rearrange("p (t k) -> p t k", t=4),
-                              in_=x[:, 1024 * gp:1024 * gp + 1024].rearrange("(t p) k -> p t k", p=P))
-            raws.append(raw)
+                              in_=w_out[512 * oc:512 * oc + 512, 1024 * cp:1024 * cp + 1024].rearrange("(t p) k -> p t k", p=P))
+
+        load_x(0)
+        load_in(0)
+        load_in(1)
         with nc.allow_non_contiguous_dma(reason="small coefficient tables"):
             for arr in range(2):
-                nc.scalar.dma_start(out=V0[8 * arr:8 * arr + 8, :],
+                nc.gpsimd.dma_start(out=V0[8 * arr:8 * arr + 8, :],
                                     in_=pads[arr][0:1, :].rearrange("o (h c) -> (o h) c", c=P))
+                nc.gpsimd.dma_start(out=V0[16 + 3 * arr:19 + 3 * arr, 0:4], in_=pads[arr][8:11, 0:4])
             for i in range(7):
                 n = 64 >> i
                 off = P - 2 * n
                 for arr in range(2):
                     r0 = 56 * arr + 8 * i
-                    nc.scalar.dma_start(out=U[r0:r0 + 8, off:off + n],
-                                        in_=pads[arr][i + 1:i + 2, 0:8 * n].rearrange("o (h q) -> (o h) q", q=n))
-            for arr in range(2):
-                for l in range(3):
-                    nc.gpsimd.dma_start(out=hcb[:, 3 * arr + l, 0:4],
-                                        in_=pads[arr][8 + l:9 + l, 0:4].rearrange("o j -> (o j)").partition_broadcast(P))
-        for h in range(8):
-            raw = rawp.tile([P, 4096], BF16, name="raw", tag="raw")
-            nc.sync.dma_start(out=raw[:], in_=w_in[256 * h:256 * h + 256, :].rearrange("(p e) k -> p (e k)", e=2))
-            raws.append(raw)
-        for oc in range(4):
-            for cp in range(2):
-                raw = rawp.tile([P, 4096], BF16, name="raw", tag="raw")
-                nc.sync.dma_start(out=raw[:].rearrange("p (t k) -> p t k", t=4),
-                                  in_=w_out[512 * oc:512 * oc + 512, 1024 * cp:1024 * cp + 1024].rearrange("(t p) k -> p t k", p=P))
-                raws.append(raw)
+                    q = nc.sync if i < 3 else nc.gpsimd
+                    q.dma_start(out=U[r0:r0 + 8, off:off + n],
+                                in_=pads[arr][i + 1:i + 2, 0:8 * n].rearrange("o (h q) -> (o h) q", q=n))
+        for h in range(2, 6):
+            load_in(h)
+        load_x(1)
+        load_in(6)
+        load_in(7)
+        for un in range(8):
+            load_out(un)
         bias = const.tile([P, 2048], BF16, name="bias")
         nc.sync.dma_start(out=bias[:], in_=b_out.partition_broadcast(P))
 
-        def prepare(raw, codes, scales, moving, copies):
+        def turn(raw, kind, copies):
             rawW = raw[:].bitcast(F32)
             grp = grpp.tile([P, 4096], BF16, name="grp", tag="grp", align_bytes=64)
             grpW = grp[:].bitcast(F32)
-            for a in range(2):
-                for b2 in range(2):
-                    bank = tps.tile([P, 512], F32, name="bank", tag="tp")
-                    for u in range(2):
-                        for s in range(2):
-                            if moving:
-                                src = (2 * b2 + s) * 512 + 256 * a + 128 * u
-                            else:
-                                src = a * 1024 + 256 * (2 * b2 + s) + 128 * u
-                            d = u * 256 + s * 128
-                            nc.tensor.transpose(bank[:, d:d + 128], rawW[:, src:src + 128], identF[:])
-                    dst = (a * 512 + b2 * 256) * 2
-                    copies[2 * a + b2](out=grpW[:, dst:dst + 512].rearrange("p (c u) -> p c u", u=2),
-                                       in_=bank[:].rearrange("p (u c) -> p c u", u=2))
+            for b in range(4):
+                bank = tps.tile([P, 512], F32, name="bank", tag="tp")
+                for u in range(2):
+                    for s in range(2):
+                        if kind == "out":
+                            src = (2 * (b % 2) + s) * 512 + 256 * (b // 2) + 128 * u
+                        elif kind == "in":
+                            src = (b // 2) * 1024 + 256 * (2 * (b % 2) + s) + 128 * u
+                        else:
+                            src = s * 1024 + 256 * b + 128 * u
+                        d = u * 256 + s * 128
+                        nc.tensor.transpose(bank[:, d:d + 128], rawW[:, src:src + 128], identF[:])
+                copies[b](out=grpW[:, 512 * b:512 * b + 512].rearrange("p (c u) -> p c u", u=2),
+                          in_=bank[:].rearrange("p (u c) -> p c u", u=2))
+            return grp
+
+        def quantise(grp, codes, scales):
             nc.vector.quantize_mx(out=codes.bitcast(FP8X4), scales=scales, in_=grp[:])
 
-        sc = nc.scalar.copy
-        vc = nc.vector.tensor_copy
+        xq = [const.tile([P, 1024], U32, name="xq%d" % half, align_bytes=64) for half in range(2)]
+        xs = [const.tile([P, 1024], U8, name="xs%d" % half, align_bytes=64) for half in range(2)]
+        wcodes = {}
 
-        xq = const.tile([P, 2048], U32, name="xq", align_bytes=64)
-        xs = const.tile([P, 2048], U8, name="xs", align_bytes=64)
-        for gp in range(2):
-            prepare(raws[gp], xq[:, 1024 * gp:1024 * gp + 1024], xs[:, 1024 * gp:1024 * gp + 1024], True, (vc, vc, vc, vc))
+        def turn_x(half, copies):
+            return turn(raws["x", half], "x", copies)
 
-        v0ps = tps.tile([P, P], BF16, name="v0ps", tag="tp")
-        nc.tensor.transpose(v0ps[:], V0[:], identB[:])
-        c0 = const.tile([P, 16], F32, name="c0")
-        nc.vector.tensor_copy(out=c0[:], in_=v0ps[:, 0:16])
+        def quantise_x(half, grp):
+            quantise(grp, xq[half][:], xs[half][:])
 
-        ups = tps.tile([P, P], BF16, name="ups", tag="tp")
-        nc.tensor.transpose(ups[:], U[:], identB[:])
-        R = const.tile([P, 2, 56, 2], BF16, name="R")
-        nc.vector.tensor_copy(out=R[:, 0, :, 0], in_=ups[:, 0:56])
-        nc.vector.tensor_scalar_mul(out=R[:, 0, :, 1], in0=ups[:, 56:112], scalar1=-1.0)
-        nc.vector.tensor_copy(out=R[:, 1, :, 0], in_=ups[:, 56:112])
-        nc.vector.tensor_copy(out=R[:, 1, :, 1], in_=ups[:, 0:56])
+        def turn_w(k, copies):
+            return turn(raws[k], "in" if k < 8 else "out", copies)
+
+        def quantise_w(k, grp):
+            wq = wqp.tile([P, 1024], U32, name="wq", tag="wq", align_bytes=64)
+            ws = wqp.tile([P, 1024], U8, name="ws", tag="ws", align_bytes=64)
+            quantise(grp, wq[:], ws[:])
+            wcodes[k] = (wq, ws)
+
+        accs = {}
+        t0s = {}
+        s0s = {}
+
+        def first(k):
+            half, h = k // 8, k % 8
+            wq, ws = wcodes[h]
+            acc = accp.tile([P, 512], F32, name="acc", tag="acc")
+            for e in range(2):
+                for g in range(4):
+                    c = (4 * e + g) * 128
+                    m = HALF * g
+                    nc.tensor.matmul_mx(out=acc[:, HALF * e:HALF * e + HALF], lhsT=wq[:, c:c + 128].bitcast(FP8X4), lhsT_scale=ws[:, c:c + 128],
+                                        rhs=xq[half][:, m:m + HALF].bitcast(FP8X4), rhs_scale=xs[half][:, m:m + HALF],
+                                        start=(g == 0), stop=(g == 3))
+            accs[k] = acc
+
+        def stage0_products(k):
+            h = k % 8
+            acc = accs[k]
+            t = k2.tile([P, 512], F32, name="t0", tag="t", align_bytes=64)
+            nc.scalar.activation(out=t[:, 0:HALF], in_=acc[:, HALF:512], func=ACTF.Copy, scale=c0[:, 8 + h:9 + h])
+            nc.scalar.activation(out=t[:, HALF:512], in_=acc[:, 0:HALF], func=ACTF.Copy, scale=c0[:, 16 + h:17 + h])
+            t0s[k] = t
+
+        def stage0_sums(k):
+            h = k % 8
+            s0 = s0p.tile([P, 512], F32, name="s0", tag="s0", align_bytes=64)
+            nc.vector.scalar_tensor_tensor(out=s0[:], in0=accs[k][:], scalar=c0[:, h:h + 1], in1=t0s[k][:], op0=ALU.mult, op1=ALU.add)
+            s0s[k] = s0
+
+        ys = [const.tile([P, 4, 1024], F32, name="y%d" % half, align_bytes=64) for half in range(2)]
+        lbs = {}
+        t8s = {}
+
+        def middle(n):
+            half, j, bt = n // 8, (n // 2) % 4, n % 2
+            lb = accp.tile([P, 512], F32, name="lb", tag="acc")
+            for hl in range(2):
+                h = 2 * j + hl
+                nc.tensor.matmul(out=lb[:, 256 * hl:256 * hl + 256], lhsT=LT[:, h, :],
+                                 rhs=s0s[8 * half + h][:].rearrange("p (e t b) -> p e t b", e=2, t=2)[:, :, bt, :], start=True, stop=True)
+            lbs[n] = lb
+
+        def stage8_products(n):
+            j = (n // 2) % 4
+            lb = lbs[n]
+            t = k2.tile([P, 512], F32, name="t8", tag="t", align_bytes=64)
+            nc.scalar.activation(out=t[:, 0:256], in_=lb[:, 256:512], func=ACTF.Copy, scale=hc[:, j, 3:4])
+            nc.scalar.activation(out=t[:, 256:512], in_=lb[:, 0:256], func=ACTF.Copy, scale=hn[:, j:j + 1])
+            t8s[n] = t
+
+        def stage8_sums(n):
+            half, j, bt = n // 8, (n // 2) % 4, n % 2
+            nc.vector.scalar_tensor_tensor(out=ys[half][:, j, 512 * bt:512 * bt + 512].rearrange("p (b t) -> p b t", t=4),
+                                           in0=lbs[n][:].rearrange("p (t b) -> p b t", t=4), scalar=hc[:, j, 0:1],
+                                           in1=t8s[n][:].rearrange("p (t b) -> p b t", t=4), op0=ALU.mult, op1=ALU.add)
+
+        t9s = {}
+
+        def stage9_products(n):
+            half, j2, bt = n // 4, (n // 2) % 2, n % 2
+            t = k4.tile([P, 2, 512], F32, name="t9", tag="t4k", align_bytes=64)
+            nc.scalar.activation(out=t[:], in_=ys[half][:, 2 * j2:2 * j2 + 2, 512 * bt:512 * bt + 512], func=ACTF.Copy, scale=hc[:, j2, 4:5])
+            t9s[n] = t
+
+        def stage9_sums(n):
+            half, j2, bt = n // 4, (n // 2) % 2, n % 2
+            cols = slice(512 * bt, 512 * bt + 512)
+            y = ys[half]
+            t = t9s[n]
+            x0 = y[:, 2 * j2, cols]
+            x1 = y[:, 2 * j2 + 1, cols]
+            nc.vector.scalar_tensor_tensor(out=x0, in0=x0, scalar=hc[:, j2, 1:2], in1=t[:, 1, :], op0=ALU.mult, op1=ALU.add)
+            nc.vector.scalar_tensor_tensor(out=x1, in0=x1, scalar=hc[:, j2, 1:2], in1=t[:, 0, :], op0=ALU.mult, op1=ALU.subtract)
+
+        ggs = {}
+        t10s = {}
+        gqs = {}
+
+        def stage10_products(bt, c):
+            t = k4.tile([P, 2, 512], F32, name="t10", tag="t4k", align_bytes=64)
+            nc.scalar.activation(out=t[:], in_=ys[bt // 2][:, c::2, 512 * (bt % 2):512 * (bt % 2) + 512], func=ACTF.Copy, scale=hc[:, 0, 5:6])
+            t10s[bt, c] = t
+
+        def stage10_sums(bt, c):
+            if c == 0:
+                ggs[bt] = ggp.tile([P, 4, 512], BF16, name="gg", tag="gg", align_bytes=64)
+            gg = ggs[bt]
+            t = t10s[bt, c]
+            cols = slice(512 * (bt % 2), 512 * (bt % 2) + 512)
+            y = ys[bt // 2]
+            nc.vector.scalar_tensor_tensor(out=gg[:, c, :], in0=y[:, c, cols], scalar=hc[:, 0, 2:3], in1=t[:, 1, :], op0=ALU.mult, op1=ALU.add)
+            nc.vector.scalar_tensor_tensor(out=gg[:, c + 2, :], in0=y[:, c + 2, cols], scalar=hc[:, 0, 2:3], in1=t[:, 0, :], op0=ALU.mult, op1=ALU.subtract)
+
+        def quantise_g(bt):
+            gq = gqp.tile([P, 512], U32, name="gq", tag="gq", align_bytes=64)
+            gs = gqp.tile([P, 512], U8, name="gs", tag="gs", align_bytes=64)
+            nc.vector.quantize_mx(out=gq[:].bitcast(FP8X4), scales=gs[:], in_=ggs[bt][:].rearrange("p c n -> p (c n)"))
+            gqs[bt] = (gq, gs)
+
+        acc2 = {}
+
+        def second(m):
+            bt, oc = m // 4, m % 4
+            gq, gs = gqs[bt]
+            acc = accp.tile([P, 512], F32, name="acc2", tag="acc")
+            for c in range(4):
+                wq, ws = wcodes[8 + 2 * oc + c // 2]
+                r = 512 * (c % 2)
+                nc.tensor.matmul_mx(out=acc[:], lhsT=gq[:, 128 * c:128 * c + 128].bitcast(FP8X4), lhsT_scale=gs[:, 128 * c:128 * c + 128],
+                                    rhs=wq[:, r:r + 512].bitcast(FP8X4), rhs_scale=ws[:, r:r + 512],
+                                    start=(c == 0), stop=(c == 3))
+            acc2[m] = acc
+
+        def leave(m):
+            bt, oc = m // 4, m % 4
+            osb = osp.tile([P, 512], F32, name="osb", tag="osb", align_bytes=64)
+            nc.vector.tensor_tensor(out=osb[:], in0=acc2[m][:], in1=bias[:, 512 * oc:512 * oc + 512], op=ALU.add)
+            nc.sync.dma_start(out=out[128 * bt:128 * bt + 128, 512 * oc:512 * oc + 512], in_=osb[:])
+
+        identB = const.tile([P, P], BF16, name="identB")
+        nc.vector.tensor_copy(out=identB[:], in_=identF[:])
+        ET = const.tile([P, 2, P], F32, name="ET")
+        nc.vector.memset(ET[:], 0.0)
+        for i in range(7):
+            n = 64 >> i
+            off = P - 2 * n
+            if i == 0:
+                nc.vector.tensor_copy(out=ET[:, :, off:off + n].rearrange("p z q -> p q z"), in_=identF[:].rearrange("p (q z) -> p q z", z=2))
+            else:
+                nc.vector.tensor_reduce(out=ET[:, :, off:off + n].rearrange("p z q -> p q z"),
+                                        in_=identF[:].rearrange("p (q z r) -> p q z r", z=2, r=1 << i), axis=AXIS.X, op=ALU.add)
+
+        both = (vc, sc, vc, sc)
+        grp = turn_x(0, both)
+        quantise_x(0, grp)
+        grp = turn_w(0, both)
+        quantise_w(0, grp)
 
         eps = tps.tile([P, 2, P], F32, name="eps", tag="tp")
         for z in range(2):
-            nc.tensor.transpose(eps[:, z, :], ET[:].rearrange("p (c z) -> p z c", z=2)[:, z, :], identF[:])
+            nc.tensor.transpose(eps[:, z, :], ET[:, z, :], identF[:])
+        v0ps = tps.tile([P, P], BF16, name="v0ps", tag="tp")
+        nc.tensor.transpose(v0ps[:], V0[:], identB[:])
+        hps = tps.tile([P, 4, 6], F32, name="hps", tag="tp")
+        for j in range(4):
+            nc.tensor.matmul(out=hps[:, j, :], lhsT=V0[:, j:j + 1].to_broadcast([P, P]), rhs=identB[:, 16:22], start=True, stop=True)
         E = const.tile([P, 2, P], BF16, name="E")
         nc.vector.tensor_copy(out=E[:], in_=eps[:])
-        fps = tps.tile([P, 112], F32, name="fps", tag="tp")
-        for z in range(2):
-            nc.tensor.matmul(out=fps[:], lhsT=E[:, z, :], rhs=R[:, z].rearrange("p r o -> p (r o)"),
-                             start=(z == 0), stop=(z == 1))
+        c0 = const.tile([P, 24], F32, name="c0")
+        nc.vector.tensor_copy(out=c0[:, 0:16], in_=v0ps[:, 0:16])
+        nc.vector.tensor_scalar_mul(out=c0[:, 16:24], in0=v0ps[:, 8:16], scalar1=-1.0)
+        hc = const.tile([P, 4, 6], F32, name="hc")
+        nc.vector.tensor_copy(out=hc[:], in_=hps[:])
+        hn = const.tile([P, 4], F32, name="hn")
+        nc.vector.tensor_scalar_mul(out=hn[:], in0=hc[:, :, 3], scalar1=-1.0)
+
+        grp = turn_w(1, both)
+        quantise_w(1, grp)
+        R = const.tile([P, 2, 56, 2], BF16, name="R")
         F = const.tile([P, 7, 8, 2], F32, name="F")
-        nc.vector.tensor_copy(out=F[:].rearrange("p i h o -> p (i h o)"), in_=fps[:])
-        prev = F[:, 0]
-        for i in range(1, 7):
-            r = 1 << i
-            nxt = const.tile([P, 8, 2 * r], F32, name="lt%d" % i)
-            nc.vector.tensor_tensor(out=nxt[:].rearrange("p h (o r) -> p h o r", o=2),
-                                    in0=F[:, i].unsqueeze(3).to_broadcast([P, 8, 2, r]),
-                                    in1=prev.unsqueeze(2).to_broadcast([P, 8, 2, r]), op=ALU.mult)
-            prev = nxt[:]
-        LT = prev
 
-        hc = const.tile([P, 6, 4], F32, name="hc")
-        nc.vector.tensor_copy(out=hc[:], in_=hcb[:, :, 0:4])
+        def tables_1():
+            ups = tps.tile([P, P], BF16, name="ups", tag="tp")
+            nc.tensor.transpose(ups[:], U[:], identB[:])
+            nc.vector.tensor_copy(out=R[:, 0, :, 0], in_=ups[:, 0:56])
+            nc.vector.tensor_scalar_mul(out=R[:, 0, :, 1], in0=ups[:, 56:112], scalar1=-1.0)
+            nc.vector.tensor_copy(out=R[:, 1, :, 0], in_=ups[:, 56:112])
+            nc.vector.tensor_copy(out=R[:, 1, :, 1], in_=ups[:, 0:56])
 
-        def rotate(x0, x1, ca, cb, o0, o1, pool, shape):
-            t1 = pool.tile(shape, F32, name="t1", tag="t", align_bytes=64)
-            t2 = pool.tile(shape, F32, name="t2", tag="t", align_bytes=64)
-            nc.scalar.activation(out=t1[:], in_=x1, func=ACTF.Copy, scale=cb)
-            nc.scalar.activation(out=t2[:], in_=x0, func=ACTF.Copy, scale=cb)
-            nc.vector.scalar_tensor_tensor(out=o0, in0=x0, scalar=ca, in1=t1[:], op0=ALU.mult, op1=ALU.add)
-            nc.vector.scalar_tensor_tensor(out=o1, in0=x1, scalar=ca, in1=t2[:], op0=ALU.mult, op1=ALU.subtract)
+        def tables_2():
+            fps = tps.tile([P, 112], F32, name="fps", tag="tp")
+            for z in range(2):
+                nc.tensor.matmul(out=fps[:], lhsT=E[:, z, :], rhs=R[:, z].rearrange("p r o -> p (r o)"),
+                                 start=(z == 0), stop=(z == 1))
+            nc.vector.tensor_copy(out=F[:].rearrange("p i h o -> p (i h o)"), in_=fps[:])
+            prev = F[:, 0]
+            for i in range(1, 7):
+                r = 1 << i
+                nxt = const.tile([P, 8, 2 * r], F32, name="lt%d" % i)
+                nc.vector.tensor_tensor(out=nxt[:].rearrange("p h (o r) -> p h o r", o=2),
+                                        in0=F[:, i].unsqueeze(3).to_broadcast([P, 8, 2, r]),
+                                        in1=prev.unsqueeze(2).to_broadcast([P, 8, 2, r]), op=ALU.mult)
+                prev = nxt[:]
+            return prev
 
-        y = const.tile([P, 16, 512], F32, name="y")
-        s0s = {}
-        for h in range(8):
-            wq = wqp.tile([P, 1024], U32, name="wq", tag="wq", align_bytes=64)
-            ws = wqp.tile([P, 1024], U8, name="ws", tag="ws", align_bytes=64)
-            prepare(raws[2 + h], wq[:], ws[:], False, (sc, sc, sc, sc))
-            accs = []
-            for e in range(2):
-                acc = accp.tile([P, 512], F32, name="acc", tag="acc")
-                for g in range(4):
-                    c = (4 * e + g) * 128
-                    nc.tensor.matmul_mx(out=acc[:], lhsT=wq[:, c:c + 128].bitcast(FP8X4), lhsT_scale=ws[:, c:c + 128],
-                                        rhs=xq[:, 512 * g:512 * g + 512].bitcast(FP8X4), rhs_scale=xs[:, 512 * g:512 * g + 512],
-                                        start=(g == 0), stop=(g == 3))
-                accs.append(acc)
-            s0 = k4.tile([P, 2, 512], F32, name="s0", tag="t", align_bytes=64)
-            rotate(accs[0][:], accs[1][:], c0[:, h:h + 1], c0[:, 8 + h:9 + h], s0[:, 0, :], s0[:, 1, :], k2, [P, 512])
-            s0s[h] = s0
-            if h % 2 == 1:
-                j = h // 2
-                for e in range(2):
-                    lps = []
-                    for hh in (h - 1, h):
-                        lp = accp.tile([P, 512], F32, name="lp", tag="acc")
-                        nc.tensor.matmul(out=lp[:], lhsT=LT[:, hh, :], rhs=s0s[hh][:, e, :], start=True, stop=True)
-                        lps.append(lp)
-                    rotate(lps[0][:], lps[1][:], hc[:, 0, j:j + 1], hc[:, 3, j:j + 1],
-                           y[:, 2 * (h - 1) + e, :], y[:, 2 * h + e, :], k2, [P, 512])
-            if h % 4 == 3:
-                j = h // 4
-                for hl in range(2):
-                    r0 = 8 * j + 2 * hl
-                    rotate(y[:, r0:r0 + 2, :], y[:, r0 + 4:r0 + 6, :], hc[:, 1, j:j + 1], hc[:, 4, j:j + 1],
-                           y[:, r0:r0 + 2, :], y[:, r0 + 4:r0 + 6, :], k4, [P, 2, 512])
 
-        woq = const.tile([P, 8192], U32, name="woq", align_bytes=64)
-        wos = const.tile([P, 8192], U8, name="wos", align_bytes=64)
-        for un in range(8):
-            prepare(raws[10 + un], woq[:, 1024 * un:1024 * un + 1024], wos[:, 1024 * un:1024 * un + 1024], True, (sc, sc, sc, vc))
-
-        for bt in range(4):
-            cols = slice(128 * bt, 128 * bt + 128)
-            gb = k4.tile([P, 16, 128], BF16, name="gb", tag="t", align_bytes=64)
-            rotate(y[:, 0:8, cols], y[:, 8:16, cols], hc[:, 2, 0:1], hc[:, 5, 0:1], gb[:, 0:8, :], gb[:, 8:16, :], k4, [P, 8, 128])
-            gg = k4.tile([P, 4, 128, 4], BF16, name="gg", tag="t", align_bytes=64)
-            nc.vector.tensor_copy(out=gg[:], in_=gb[:].rearrange("p (c t) b -> p c b t", t=4))
-            gq = const.tile([P, 512], U32, name="gq%d" % bt, align_bytes=64)
-            gs = const.tile([P, 512], U8, name="gs%d" % bt, align_bytes=64)
-            nc.vector.quantize_mx(out=gq[:].bitcast(FP8X4), scales=gs[:], in_=gg[:].rearrange("p c b t -> p (c b t)"))
-            for op in range(2):
-                osb = k4.tile([P, 1024], F32, name="osb", tag="t", align_bytes=64)
-                for o2 in range(2):
-                    oc = 2 * op + o2
-                    acc = accp.tile([P, 512], F32, name="acc2", tag="acc")
-                    for c in range(4):
-                        m = (4 * oc + c) * 512
-                        nc.tensor.matmul_mx(out=acc[:], lhsT=gq[:, 128 * c:128 * c + 128].bitcast(FP8X4), lhsT_scale=gs[:, 128 * c:128 * c + 128],
-                                            rhs=woq[:, m:m + 512].bitcast(FP8X4), rhs_scale=wos[:, m:m + 512],
-                                            start=(c == 0), stop=(c == 3))
-                    nc.vector.tensor_tensor(out=osb[:, 512 * o2:512 * o2 + 512], in0=acc[:], in1=bias[:, 512 * oc:512 * oc + 512], op=ALU.add)
-                nc.sync.dma_start(out=out[128 * bt:128 * bt + 128, 1024 * op:1024 * op + 1024], in_=osb[:])
+        nine = {}
+        for n in range(8):
+            nine[8 * (n // 4) + 4 * ((n // 2) % 2) + n % 2 + 6] = n
+        turns = {}
+        for n in range(2, 8):
+            turns[n - 2] = n
+        for n in range(8):
+            turns[6 + 2 * n if n < 5 else 11 + n] = 8 + n
+        pieces = {14: [0], 15: [1], 16: [4, 5], 18: [2], 19: [6], 20: [3, 7], 21: [8, 9, 10, 11], 22: [12, 13, 14, 15]}
+        left = []
+        last = None
+        for k in range(23):
+            if 3 <= k < 19:
+                stage8_products(k - 3)
+            if last is not None:
+                quantise_w(last[0], last[1])
+            if 1 <= k < 17:
+                stage0_sums(k - 1)
+            if k in nine:
+                stage9_products(nine[k])
+            if 11 <= k < 15:
+                stage10_products((k - 11) // 2, (k - 11) % 2)
+            if 3 <= k < 19:
+                stage8_sums(k - 3)
+            if k == 1:
+                tables_1()
+                LT = tables_2()
+            last = None
+            if k in turns:
+                last = (turns[k], turn_w(turns[k], (sc, sc, sc, sc)))
+            if k == 5:
+                grpx = turn_x(1, both)
+            if k < 16:
+                first(k)
+            if 2 <= k < 18:
+                middle(k - 2)
+            if k in nine:
+                stage9_sums(nine[k])
+            if k < 16:
+                stage0_products(k)
+            if 12 <= k < 16:
+                stage10_sums((k - 12) // 2, k % 2)
+                if k % 2 == 1:
+                    quantise_g((k - 12) // 2)
+            if 19 <= k < 21:
+                for c in range(2):
+                    stage10_products(k - 17, c)
+                for c in range(2):
+                    stage10_sums(k - 17, c)
+                quantise_g(k - 17)
+            for m in left:
+                leave(m)
+            left = pieces.get(k, [])
+            for m in left:
+                second(m)
+            if k == 5:
+                quantise_x(1, grpx)
+        for m in left:
+            leave(m)

@@ -32,6 +32,7 @@ def tile_butterflylayer_kernel(tc, x, w_in, w_out, b_out, a_pad, b_pad, out):
         osp = ctx.enter_context(tc.tile_pool(name="osp", bufs=5))
         tps = ctx.enter_context(tc.psum_pool(name="tps", bufs=4))
         accp = ctx.enter_context(tc.psum_pool(name="accp", bufs=4))
+        ctx.enter_context(tc.manual_schedule())
 
         sc = nc.scalar.copy
         vc = nc.vector.tensor_copy
@@ -66,6 +67,7 @@ def tile_butterflylayer_kernel(tc, x, w_in, w_out, b_out, a_pad, b_pad, out):
             nc.sync.dma_start(out=raw[:].rearrange("p (t k) -> p t k", t=4),
                               in_=w_out[512 * oc:512 * oc + 512, 1024 * cp:1024 * cp + 1024].rearrange("(t p) k -> p t k", p=P))
 
+        XB = 5
         load_x(0)
         load_in(0)
         load_in(1)
@@ -82,11 +84,10 @@ def tile_butterflylayer_kernel(tc, x, w_in, w_out, b_out, a_pad, b_pad, out):
                     q = nc.sync if i < 3 else nc.gpsimd
                     q.dma_start(out=U[r0:r0 + 8, off:off + n],
                                 in_=pads[arr][i + 1:i + 2, 0:8 * n].rearrange("o (h q) -> (o h) q", q=n))
-        for h in range(2, 6):
+        for h in range(2, 8):
             load_in(h)
-        load_x(1)
-        load_in(6)
-        load_in(7)
+            if h == XB:
+                load_x(1)
         for un in range(8):
             load_out(un)
         bias = const.tile([P, 2048], BF16, name="bias")
@@ -138,8 +139,8 @@ def tile_butterflylayer_kernel(tc, x, w_in, w_out, b_out, a_pad, b_pad, out):
         t0s = {}
         s0s = {}
 
-        def first(k):
-            half, h = k // 8, k % 8
+        def first(row):
+            half, h = row
             wq, ws = wcodes[h]
             acc = accp.tile([P, 512], F32, name="acc", tag="acc")
             for e in range(2):
@@ -149,21 +150,21 @@ def tile_butterflylayer_kernel(tc, x, w_in, w_out, b_out, a_pad, b_pad, out):
                     nc.tensor.matmul_mx(out=acc[:, HALF * e:HALF * e + HALF], lhsT=wq[:, c:c + 128].bitcast(FP8X4), lhsT_scale=ws[:, c:c + 128],
                                         rhs=xq[half][:, m:m + HALF].bitcast(FP8X4), rhs_scale=xs[half][:, m:m + HALF],
                                         start=(g == 0), stop=(g == 3))
-            accs[k] = acc
+            accs[row] = acc
 
-        def stage0_products(k):
-            h = k % 8
-            acc = accs[k]
+        def stage0_products(row):
+            h = row[1]
+            acc = accs[row]
             t = k2.tile([P, 512], F32, name="t0", tag="t", align_bytes=64)
             nc.scalar.activation(out=t[:, 0:HALF], in_=acc[:, HALF:512], func=ACTF.Copy, scale=c0[:, 8 + h:9 + h])
             nc.scalar.activation(out=t[:, HALF:512], in_=acc[:, 0:HALF], func=ACTF.Copy, scale=c0[:, 16 + h:17 + h])
-            t0s[k] = t
+            t0s[row] = t
 
-        def stage0_sums(k):
-            h = k % 8
+        def stage0_sums(row):
+            h = row[1]
             s0 = s0p.tile([P, 512], F32, name="s0", tag="s0", align_bytes=64)
-            nc.vector.scalar_tensor_tensor(out=s0[:], in0=accs[k][:], scalar=c0[:, h:h + 1], in1=t0s[k][:], op0=ALU.mult, op1=ALU.add)
-            s0s[k] = s0
+            nc.vector.scalar_tensor_tensor(out=s0[:], in0=accs[row][:], scalar=c0[:, h:h + 1], in1=t0s[row][:], op0=ALU.mult, op1=ALU.add)
+            s0s[row] = s0
 
         ys = [const.tile([P, 4, 1024], F32, name="y%d" % half, align_bytes=64) for half in range(2)]
         lbs = {}
@@ -175,7 +176,7 @@ def tile_butterflylayer_kernel(tc, x, w_in, w_out, b_out, a_pad, b_pad, out):
             for hl in range(2):
                 h = 2 * j + hl
                 nc.tensor.matmul(out=lb[:, 256 * hl:256 * hl + 256], lhsT=LT[:, h, :],
-                                 rhs=s0s[8 * half + h][:].rearrange("p (e t b) -> p e t b", e=2, t=2)[:, :, bt, :], start=True, stop=True)
+                                 rhs=s0s[half, h][:].rearrange("p (e t b) -> p e t b", e=2, t=2)[:, :, bt, :], start=True, stop=True)
             lbs[n] = lb
 
         def stage8_products(n):
@@ -274,12 +275,12 @@ def tile_butterflylayer_kernel(tc, x, w_in, w_out, b_out, a_pad, b_pad, out):
         grp = turn_w(0, both)
         quantise_w(0, grp)
 
-        eps = tps.tile([P, 2, P], F32, name="eps", tag="tp")
+        eps = accp.tile([P, 2, P], F32, name="eps", tag="acc")
         for z in range(2):
             nc.tensor.transpose(eps[:, z, :], ET[:, z, :], identF[:])
-        v0ps = tps.tile([P, P], BF16, name="v0ps", tag="tp")
+        v0ps = accp.tile([P, P], BF16, name="v0ps", tag="acc")
         nc.tensor.transpose(v0ps[:], V0[:], identB[:])
-        hps = tps.tile([P, 4, 6], F32, name="hps", tag="tp")
+        hps = accp.tile([P, 4, 6], F32, name="hps", tag="acc")
         for j in range(4):
             nc.tensor.matmul(out=hps[:, j, :], lhsT=V0[:, j:j + 1].to_broadcast([P, P]), rhs=identB[:, 16:22], start=True, stop=True)
         E = const.tile([P, 2, P], BF16, name="E")
@@ -298,7 +299,7 @@ def tile_butterflylayer_kernel(tc, x, w_in, w_out, b_out, a_pad, b_pad, out):
         F = const.tile([P, 7, 8, 2], F32, name="F")
 
         def tables_1():
-            ups = tps.tile([P, P], BF16, name="ups", tag="tp")
+            ups = accp.tile([P, P], BF16, name="ups", tag="acc")
             nc.tensor.transpose(ups[:], U[:], identB[:])
             nc.vector.tensor_copy(out=R[:, 0, :, 0], in_=ups[:, 0:56])
             nc.vector.tensor_scalar_mul(out=R[:, 0, :, 1], in0=ups[:, 56:112], scalar1=-1.0)
@@ -306,78 +307,110 @@ def tile_butterflylayer_kernel(tc, x, w_in, w_out, b_out, a_pad, b_pad, out):
             nc.vector.tensor_copy(out=R[:, 1, :, 1], in_=ups[:, 0:56])
 
         def tables_2():
-            fps = tps.tile([P, 112], F32, name="fps", tag="tp")
+            fps = accp.tile([P, 112], F32, name="fps", tag="acc")
             for z in range(2):
                 nc.tensor.matmul(out=fps[:], lhsT=E[:, z, :], rhs=R[:, z].rearrange("p r o -> p (r o)"),
                                  start=(z == 0), stop=(z == 1))
             nc.vector.tensor_copy(out=F[:].rearrange("p i h o -> p (i h o)"), in_=fps[:])
-            prev = F[:, 0]
-            for i in range(1, 7):
-                r = 1 << i
-                nxt = const.tile([P, 8, 2 * r], F32, name="lt%d" % i)
-                nc.vector.tensor_tensor(out=nxt[:].rearrange("p h (o r) -> p h o r", o=2),
-                                        in0=F[:, i].unsqueeze(3).to_broadcast([P, 8, 2, r]),
-                                        in1=prev.unsqueeze(2).to_broadcast([P, 8, 2, r]), op=ALU.mult)
-                prev = nxt[:]
-            return prev
+
+            def outer(name, high, low, n, r):
+                pair = const.tile([P, 8, n * r], F32, name=name)
+                nc.vector.tensor_tensor(out=pair[:].rearrange("p h (o r) -> p h o r", o=n),
+                                        in0=high.unsqueeze(3).to_broadcast([P, 8, n, r]),
+                                        in1=low.unsqueeze(2).to_broadcast([P, 8, n, r]), op=ALU.mult)
+                return pair[:]
+
+            f10 = outer("f10", F[:, 1], F[:, 0], 2, 2)
+            f54 = outer("f54", F[:, 5], F[:, 4], 2, 2)
+            f32 = outer("f32", F[:, 3], F[:, 2], 2, 2)
+            f654 = outer("f654", F[:, 6], f54, 2, 4)
+            f3210 = outer("f3210", f32, f10, 4, 4)
+            return outer("lt", f654, f3210, 8, 16)
 
 
-        nine = {}
-        for n in range(8):
-            nine[8 * (n // 4) + 4 * ((n // 2) % 2) + n % 2 + 6] = n
-        turns = {}
-        for n in range(2, 8):
-            turns[n - 2] = n
-        for n in range(8):
-            turns[6 + 2 * n if n < 5 else 11 + n] = 8 + n
-        pieces = {14: [0], 15: [1], 16: [4, 5], 18: [2], 19: [6], 20: [3, 7], 21: [8, 9, 10, 11], 22: [12, 13, 14, 15]}
+        LAG = 8
+        rows = []
+        for h in range(8):
+            rows.append((0, h))
+            if h >= LAG:
+                rows.append((1, h - LAG))
+        rows = rows + [(1, h) for h in range(8 - min(LAG, 8), 8)]
+        at = {}
+        for k, (half, h) in enumerate(rows):
+            at[half, h] = k
+        steps = {}
+
+        def put(k, kind, args):
+            steps.setdefault((k, kind), []).append(args)
+
+        for h in range(2, 8):
+            put(at[0, h - 2], "turn", h)
+        T0 = 13
+        for u in range(8):
+            put(T0 + u, "turn", 8 + u)
+        put(at[1, 0] - 3, "turnx", 1)
+        ready = {}
+        for half in range(2):
+            for j in range(4):
+                for bt in range(2):
+                    k = at[half, 2 * j + 1] + 1 + bt
+                    n = 8 * half + 2 * j + bt
+                    put(k, "middle", n)
+                    put(k + 1, "eight", n)
+                    if j % 2 == 1:
+                        put(k + 2, "nine", 4 * half + 2 * (j // 2) + bt)
+                    if j == 3:
+                        k = k + 3
+                        put(k, "ten", (2 * half + bt, 0))
+                        put(k + 1, "ten", (2 * half + bt, 1))
+                        ready[2 * half + bt] = k + 1
+        for oc in range(4):
+            for bt in range(4):
+                put(max(T0 + 2 * oc + 2, ready[bt] + 1), "second", 4 * bt + oc)
+        last_step = max(k for k, kind in steps)
         left = []
-        last = None
-        for k in range(23):
-            if 3 <= k < 19:
-                stage8_products(k - 3)
-            if last is not None:
-                quantise_w(last[0], last[1])
-            if 1 <= k < 17:
-                stage0_sums(k - 1)
-            if k in nine:
-                stage9_products(nine[k])
-            if 11 <= k < 15:
-                stage10_products((k - 11) // 2, (k - 11) % 2)
-            if 3 <= k < 19:
-                stage8_sums(k - 3)
-            if k == 1:
-                tables_1()
-                LT = tables_2()
-            last = None
-            if k in turns:
-                last = (turns[k], turn_w(turns[k], (sc, sc, sc, sc)))
-            if k == 5:
+        last = []
+        for k in range(last_step + 1):
+            for n in steps.get((k, "eight"), []):
+                stage8_products(n)
+            for u, grp in last:
+                quantise_w(u, grp)
+            if 1 <= k <= 16:
+                stage0_sums(rows[k - 1])
+            for n in steps.get((k, "nine"), []):
+                stage9_products(n)
+            for bt, c in steps.get((k, "ten"), []):
+                stage10_products(bt, c)
+            for n in steps.get((k, "eight"), []):
+                stage8_sums(n)
+            last = []
+            for u in steps.get((k, "turn"), []):
+                last.append((u, turn_w(u, (sc, sc, sc, sc))))
+            grpx = None
+            if (k, "turnx") in steps:
                 grpx = turn_x(1, both)
+            if k == 1:
+                LT = tables_2()
             if k < 16:
-                first(k)
-            if 2 <= k < 18:
-                middle(k - 2)
-            if k in nine:
-                stage9_sums(nine[k])
+                first(rows[k])
+            if k == 0:
+                tables_1()
+            for n in steps.get((k, "middle"), []):
+                middle(n)
+            for n in steps.get((k, "nine"), []):
+                stage9_sums(n)
             if k < 16:
-                stage0_products(k)
-            if 12 <= k < 16:
-                stage10_sums((k - 12) // 2, k % 2)
-                if k % 2 == 1:
-                    quantise_g((k - 12) // 2)
-            if 19 <= k < 21:
-                for c in range(2):
-                    stage10_products(k - 17, c)
-                for c in range(2):
-                    stage10_sums(k - 17, c)
-                quantise_g(k - 17)
+                stage0_products(rows[k])
+            for bt, c in steps.get((k, "ten"), []):
+                stage10_sums(bt, c)
+                if c == 1:
+                    quantise_g(bt)
             for m in left:
                 leave(m)
-            left = pieces.get(k, [])
+            left = steps.get((k, "second"), [])
             for m in left:
                 second(m)
-            if k == 5:
+            if grpx is not None:
                 quantise_x(1, grpx)
         for m in left:
             leave(m)

@@ -43,6 +43,8 @@ def tile_butterflylayer_kernel(tc, x, w_in, w_out, b_out, a_pad, b_pad, out):
         nc.vector.memset(V0[:], 0.0)
         U = const.tile([P, P], BF16, name="U")
         nc.vector.memset(U[:], 0.0)
+        V1 = const.tile([P, 4], BF16, name="V1")
+        nc.vector.memset(V1[:], 0.0)
 
         raws = {}
 
@@ -71,21 +73,30 @@ def tile_butterflylayer_kernel(tc, x, w_in, w_out, b_out, a_pad, b_pad, out):
         load_x(0)
         load_in(0)
         load_in(1)
-        with nc.allow_non_contiguous_dma(reason="small coefficient tables"):
+
+        def load_table(queue, i):
+            n = 64 >> i
+            off = P - 2 * n
             for arr in range(2):
-                nc.gpsimd.dma_start(out=V0[8 * arr:8 * arr + 8, :],
-                                    in_=pads[arr][0:1, :].rearrange("o (h c) -> (o h) c", c=P))
-                nc.gpsimd.dma_start(out=V0[16 + 3 * arr:19 + 3 * arr, 0:4], in_=pads[arr][8:11, 0:4])
-            for i in range(7):
-                n = 64 >> i
-                off = P - 2 * n
-                for arr in range(2):
-                    r0 = 56 * arr + 8 * i
-                    q = nc.sync if i < 3 else nc.gpsimd
-                    q.dma_start(out=U[r0:r0 + 8, off:off + n],
+                r0 = 56 * arr + 8 * i
+                queue.dma_start(out=U[r0:r0 + 8, off:off + n],
                                 in_=pads[arr][i + 1:i + 2, 0:8 * n].rearrange("o (h q) -> (o h) q", q=n))
+
+        ctx.enter_context(nc.allow_non_contiguous_dma(reason="small coefficient tables"))
+        for arr in range(2):
+            nc.gpsimd.dma_start(out=V0[8 * arr:8 * arr + 8, :],
+                                in_=pads[arr][0:1, :].rearrange("o (h c) -> (o h) c", c=P))
+        for i in range(3):
+            load_table(nc.scalar, i)
+        for i in range(5, 7):
+            load_table(nc.gpsimd, i)
+        for arr in range(2):
+            nc.gpsimd.dma_start(out=V1[3 * arr:3 * arr + 3, :], in_=pads[arr][8:11, 0:4])
         for h in range(2, 8):
             load_in(h)
+            if h == 3:
+                for i in range(3, 5):
+                    load_table(nc.sync, i)
             if h == XB:
                 load_x(1)
         for un in range(8):
@@ -280,18 +291,13 @@ def tile_butterflylayer_kernel(tc, x, w_in, w_out, b_out, a_pad, b_pad, out):
             nc.tensor.transpose(eps[:, z, :], ET[:, z, :], identF[:])
         v0ps = accp.tile([P, P], BF16, name="v0ps", tag="acc")
         nc.tensor.transpose(v0ps[:], V0[:], identB[:])
-        hps = accp.tile([P, 4, 6], F32, name="hps", tag="acc")
-        for j in range(4):
-            nc.tensor.matmul(out=hps[:, j, :], lhsT=V0[:, j:j + 1].to_broadcast([P, P]), rhs=identB[:, 16:22], start=True, stop=True)
         E = const.tile([P, 2, P], BF16, name="E")
         nc.vector.tensor_copy(out=E[:], in_=eps[:])
         c0 = const.tile([P, 24], F32, name="c0")
         nc.vector.tensor_copy(out=c0[:, 0:16], in_=v0ps[:, 0:16])
         nc.vector.tensor_scalar_mul(out=c0[:, 16:24], in0=v0ps[:, 8:16], scalar1=-1.0)
         hc = const.tile([P, 4, 6], F32, name="hc")
-        nc.vector.tensor_copy(out=hc[:], in_=hps[:])
         hn = const.tile([P, 4], F32, name="hn")
-        nc.vector.tensor_scalar_mul(out=hn[:], in0=hc[:, :, 3], scalar1=-1.0)
 
         grp = turn_w(1, both)
         quantise_w(1, grp)
@@ -307,6 +313,11 @@ def tile_butterflylayer_kernel(tc, x, w_in, w_out, b_out, a_pad, b_pad, out):
             nc.vector.tensor_copy(out=R[:, 1, :, 1], in_=ups[:, 0:56])
 
         def tables_2():
+            hps = accp.tile([P, 4, 6], F32, name="hps", tag="acc")
+            for j in range(4):
+                nc.tensor.matmul(out=hps[:, j, :], lhsT=V1[:, j:j + 1].to_broadcast([P, P]), rhs=identB[:, 0:6], start=True, stop=True)
+            nc.vector.tensor_copy(out=hc[:], in_=hps[:])
+            nc.vector.tensor_scalar_mul(out=hn[:], in0=hc[:, :, 3], scalar1=-1.0)
             fps = accp.tile([P, 112], F32, name="fps", tag="acc")
             for z in range(2):
                 nc.tensor.matmul(out=fps[:], lhsT=E[:, z, :], rhs=R[:, z].rearrange("p r o -> p (r o)"),
@@ -373,8 +384,6 @@ def tile_butterflylayer_kernel(tc, x, w_in, w_out, b_out, a_pad, b_pad, out):
         for k in range(last_step + 1):
             for n in steps.get((k, "eight"), []):
                 stage8_products(n)
-            for u, grp in last:
-                quantise_w(u, grp)
             if 1 <= k <= 16:
                 stage0_sums(rows[k - 1])
             for n in steps.get((k, "nine"), []):
@@ -383,7 +392,11 @@ def tile_butterflylayer_kernel(tc, x, w_in, w_out, b_out, a_pad, b_pad, out):
                 stage10_products(bt, c)
             for n in steps.get((k, "eight"), []):
                 stage8_sums(n)
+            for u, grp in last:
+                quantise_w(u, grp)
             last = []
+            if k == 0:
+                first(rows[0])
             for u in steps.get((k, "turn"), []):
                 last.append((u, turn_w(u, (sc, sc, sc, sc))))
             grpx = None
@@ -391,7 +404,7 @@ def tile_butterflylayer_kernel(tc, x, w_in, w_out, b_out, a_pad, b_pad, out):
                 grpx = turn_x(1, both)
             if k == 1:
                 LT = tables_2()
-            if k < 16:
+            if 1 <= k < 16:
                 first(rows[k])
             if k == 0:
                 tables_1()

@@ -21,12 +21,12 @@ def tile_butterflylayer_kernel(tc, x, w_in, w_out, b_out, a_pad, b_pad, out):
     pads = (a_pad, b_pad)
     with ExitStack() as ctx:
         const = ctx.enter_context(tc.tile_pool(name="const", bufs=1))
-        rawp = ctx.enter_context(tc.tile_pool(name="rawp", bufs=5))
+        rawp = ctx.enter_context(tc.tile_pool(name="rawp", bufs=6))
         grpp = ctx.enter_context(tc.tile_pool(name="grpp", bufs=3))
         wqp = ctx.enter_context(tc.tile_pool(name="wqp", bufs=10))
         k2 = ctx.enter_context(tc.tile_pool(name="k2", bufs=4))
-        s0p = ctx.enter_context(tc.tile_pool(name="s0p", bufs=6))
-        k4 = ctx.enter_context(tc.tile_pool(name="k4", bufs=4))
+        s0p = ctx.enter_context(tc.tile_pool(name="s0p", bufs=5))
+        k4 = ctx.enter_context(tc.tile_pool(name="k4", bufs=3))
         ggp = ctx.enter_context(tc.tile_pool(name="ggp", bufs=2))
         gqp = ctx.enter_context(tc.tile_pool(name="gqp", bufs=4))
         osp = ctx.enter_context(tc.tile_pool(name="osp", bufs=5))
@@ -69,7 +69,7 @@ def tile_butterflylayer_kernel(tc, x, w_in, w_out, b_out, a_pad, b_pad, out):
             nc.sync.dma_start(out=raw[:].rearrange("p (t k) -> p t k", t=4),
                               in_=w_out[512 * oc:512 * oc + 512, 1024 * cp:1024 * cp + 1024].rearrange("(t p) k -> p t k", p=P))
 
-        XB = 5
+        XB = 6
         load_x(0)
         load_in(0)
         load_in(1)
@@ -99,10 +99,10 @@ def tile_butterflylayer_kernel(tc, x, w_in, w_out, b_out, a_pad, b_pad, out):
                     load_table(nc.sync, i)
             if h == XB:
                 load_x(1)
-        for un in range(8):
-            load_out(un)
         bias = const.tile([P, 2048], BF16, name="bias")
         nc.sync.dma_start(out=bias[:], in_=b_out.partition_broadcast(P))
+        for un in range(8):
+            load_out(un)
 
         def turn(raw, kind, copies):
             rawW = raw[:].bitcast(F32)

@@ -180,6 +180,8 @@ def tile_butterflylayer_kernel(tc, x, w_in, w_out, b_out, a_pad, b_pad, out):
         ys = [const.tile([P, 4, 1024], F32, name="y%d" % half, align_bytes=64) for half in range(2)]
         lbs = {}
         t8s = {}
+        done8 = set()
+        done9 = set()
 
         def middle(n):
             half, j, bt = n // 8, (n // 2) % 4, n % 2
@@ -200,6 +202,7 @@ def tile_butterflylayer_kernel(tc, x, w_in, w_out, b_out, a_pad, b_pad, out):
 
         def stage8_sums(n):
             half, j, bt = n // 8, (n // 2) % 4, n % 2
+            done8.add(n)
             nc.vector.scalar_tensor_tensor(out=ys[half][:, j, 512 * bt:512 * bt + 512].rearrange("p (b t) -> p b t", t=4),
                                            in0=lbs[n][:].rearrange("p (t b) -> p b t", t=4), scalar=hc[:, j, 0:1],
                                            in1=t8s[n][:].rearrange("p (t b) -> p b t", t=4), op0=ALU.mult, op1=ALU.add)
@@ -208,12 +211,14 @@ def tile_butterflylayer_kernel(tc, x, w_in, w_out, b_out, a_pad, b_pad, out):
 
         def stage9_products(n):
             half, j2, bt = n // 4, (n // 2) % 2, n % 2
+            assert 8 * half + 4 * j2 + bt in done8 and 8 * half + 4 * j2 + 2 + bt in done8
             t = k4.tile([P, 2, 512], F32, name="t9", tag="t4k", align_bytes=64)
             nc.scalar.activation(out=t[:], in_=ys[half][:, 2 * j2:2 * j2 + 2, 512 * bt:512 * bt + 512], func=ACTF.Copy, scale=hc[:, j2, 4:5])
             t9s[n] = t
 
         def stage9_sums(n):
             half, j2, bt = n // 4, (n // 2) % 2, n % 2
+            done9.add(n)
             cols = slice(512 * bt, 512 * bt + 512)
             y = ys[half]
             t = t9s[n]
@@ -227,6 +232,7 @@ def tile_butterflylayer_kernel(tc, x, w_in, w_out, b_out, a_pad, b_pad, out):
         gqs = {}
 
         def stage10_products(bt, c):
+            assert 4 * (bt // 2) + bt % 2 in done9 and 4 * (bt // 2) + 2 + bt % 2 in done9
             t = k4.tile([P, 2, 512], F32, name="t10", tag="t4k", align_bytes=64)
             nc.scalar.activation(out=t[:], in_=ys[bt // 2][:, c::2, 512 * (bt % 2):512 * (bt % 2) + 512], func=ACTF.Copy, scale=hc[:, 0, 5:6])
             t10s[bt, c] = t
@@ -339,27 +345,22 @@ def tile_butterflylayer_kernel(tc, x, w_in, w_out, b_out, a_pad, b_pad, out):
             return outer("lt", f654, f3210, 8, 16)
 
 
-        LAG = 8
-        rows = []
-        for h in range(8):
-            rows.append((0, h))
-            if h >= LAG:
-                rows.append((1, h - LAG))
-        rows = rows + [(1, h) for h in range(8 - min(LAG, 8), 8)]
+        rows = [(half, h) for half in range(2) for h in range(8)]
         at = {}
-        for k, (half, h) in enumerate(rows):
-            at[half, h] = k
+        for k, row in enumerate(rows):
+            at[row] = k
         steps = {}
+        done = set()
 
         def put(k, kind, args):
             steps.setdefault((k, kind), []).append(args)
 
         for h in range(2, 8):
             put(at[0, h - 2], "turn", h)
-        T0 = 13
+        T0 = 15
         for u in range(8):
-            put(T0 + u, "turn", 8 + u)
-        put(at[1, 0] - 3, "turnx", 1)
+            put(T0 + (u * 5) // 4, "turn", 8 + u)
+        put(6, "turnx", 1)
         ready = {}
         for half in range(2):
             for j in range(4):
@@ -369,39 +370,68 @@ def tile_butterflylayer_kernel(tc, x, w_in, w_out, b_out, a_pad, b_pad, out):
                     put(k, "middle", n)
                     put(k + 1, "eight", n)
                     if j % 2 == 1:
-                        put(k + 2, "nine", 4 * half + 2 * (j // 2) + bt)
+                        put(k + (2, 2)[half], "nine", 4 * half + 2 * (j // 2) + bt)
                     if j == 3:
-                        k = k + 3
+                        k = k + (4, 4)[half] + bt * (0, 1)[half]
                         put(k, "ten", (2 * half + bt, 0))
-                        put(k + 1, "ten", (2 * half + bt, 1))
-                        ready[2 * half + bt] = k + 1
+                        k = k + (2, 1)[half]
+                        put(k, "ten", (2 * half + bt, 1))
+                        ready[2 * half + bt] = k
         for oc in range(4):
             for bt in range(4):
-                put(max(T0 + 2 * oc + 2, ready[bt] + 1), "second", 4 * bt + oc)
+                put(max(T0 + ((2 * oc + 1) * 5) // 4 + 2, ready[bt] + 1), "second", 4 * bt + oc)
         last_step = max(k for k, kind in steps)
         left = []
         last = []
         for k in range(last_step + 1):
+            late = k >= 99
+            pq = (1, 4)[late]
+            pl = (0, 4)[late]
+            pp = (0, 1)[late]
+
+            def vec(pos):
+                if pos == pq:
+                    for u, grp in last:
+                        quantise_w(u, grp)
+                if pos == pl:
+                    for m in left:
+                        leave(m)
+
             for n in steps.get((k, "eight"), []):
                 stage8_products(n)
+            vec(0)
             if 1 <= k <= 16:
                 stage0_sums(rows[k - 1])
-            for n in steps.get((k, "nine"), []):
-                stage9_products(n)
-            for bt, c in steps.get((k, "ten"), []):
-                stage10_products(bt, c)
+            vec(1)
+            if pp == 0:
+                for n in steps.get((k, "nine"), []):
+                    stage9_products(n)
+                for bt, c in steps.get((k, "ten"), []):
+                    stage10_products(bt, c)
             for n in steps.get((k, "eight"), []):
                 stage8_sums(n)
-            for u, grp in last:
-                quantise_w(u, grp)
-            last = []
+            vec(2)
+            if late and True:
+                if pp == 1:
+                    for n in steps.get((k, "nine"), []):
+                        stage9_products(n)
+                    for bt, c in steps.get((k, "ten"), []):
+                        stage10_products(bt, c)
+                for n in steps.get((k, "nine"), []):
+                    stage9_sums(n)
+                for bt, c in steps.get((k, "ten"), []):
+                    stage10_sums(bt, c)
+                    if c == 1:
+                        quantise_g(bt)
+                vec(3)
+            turned = []
             if k == 0:
                 first(rows[0])
             for u in steps.get((k, "turn"), []):
-                last.append((u, turn_w(u, (sc, sc, sc, sc))))
+                turned.append((u, turn_w(u, (sc, sc, sc, sc) if k < 0 or k >= 0 else (sc, sc, sc, vc))))
             grpx = None
             if (k, "turnx") in steps:
-                grpx = turn_x(1, both)
+                grpx = turn_x(1, (sc, sc, sc, sc))
             if k == 1:
                 LT = tables_2()
             if 1 <= k < 16:
@@ -410,17 +440,29 @@ def tile_butterflylayer_kernel(tc, x, w_in, w_out, b_out, a_pad, b_pad, out):
                 tables_1()
             for n in steps.get((k, "middle"), []):
                 middle(n)
-            for n in steps.get((k, "nine"), []):
-                stage9_sums(n)
+            if not (late and True):
+                if pp == 1:
+                    for n in steps.get((k, "nine"), []):
+                        stage9_products(n)
+                    for bt, c in steps.get((k, "ten"), []):
+                        stage10_products(bt, c)
+                for n in steps.get((k, "nine"), []):
+                    stage9_sums(n)
+                vec(3)
             if k < 16:
                 stage0_products(rows[k])
-            for bt, c in steps.get((k, "ten"), []):
-                stage10_sums(bt, c)
-                if c == 1:
-                    quantise_g(bt)
-            for m in left:
-                leave(m)
+            if not (late and True):
+                for bt, c in steps.get((k, "ten"), []):
+                    stage10_sums(bt, c)
+                    if c == 1 and False:
+                        quantise_g(bt)
+            vec(4)
+            if not (late and True) and not False:
+                for bt, c in steps.get((k, "ten"), []):
+                    if c == 1:
+                        quantise_g(bt)
             left = steps.get((k, "second"), [])
+            last = turned
             for m in left:
                 second(m)
             if grpx is not None:

@@ -37,6 +37,9 @@ def tile_butterflylayer_kernel(tc, x, w_in, w_out, b_out, a_pad, b_pad, out):
         sc = nc.scalar.copy
         vc = nc.vector.tensor_copy
 
+        spark = const.tile([P, 1], F32, name="spark")
+        nc.vector.memset(spark[:], 0.0)
+        nc.scalar.activation(out=spark[:], in_=spark[:], func=ACTF.Copy, scale=1.0)
         identF = const.tile([P, P], F32, name="identF")
         make_identity(nc, identF[:])
         V0 = const.tile([P, P], BF16, name="V0")
@@ -72,7 +75,6 @@ def tile_butterflylayer_kernel(tc, x, w_in, w_out, b_out, a_pad, b_pad, out):
         XB = 6
         load_x(0)
         load_in(0)
-        load_in(1)
 
         def load_table(queue, i):
             n = 64 >> i
@@ -92,9 +94,9 @@ def tile_butterflylayer_kernel(tc, x, w_in, w_out, b_out, a_pad, b_pad, out):
             load_table(nc.gpsimd, i)
         for arr in range(2):
             nc.gpsimd.dma_start(out=V1[3 * arr:3 * arr + 3, :], in_=pads[arr][8:11, 0:4])
-        for h in range(2, 8):
+        for h in range(1, 8):
             load_in(h)
-            if h == 3:
+            if h == 2:
                 for i in range(3, 5):
                     load_table(nc.sync, i)
             if h == XB:
@@ -197,7 +199,7 @@ def tile_butterflylayer_kernel(tc, x, w_in, w_out, b_out, a_pad, b_pad, out):
             lb = lbs[n]
             t = k2.tile([P, 512], F32, name="t8", tag="t", align_bytes=64)
             nc.scalar.activation(out=t[:, 0:256], in_=lb[:, 256:512], func=ACTF.Copy, scale=hc[:, j, 3:4])
-            nc.scalar.activation(out=t[:, 256:512], in_=lb[:, 0:256], func=ACTF.Copy, scale=hn[:, j:j + 1])
+            nc.scalar.activation(out=t[:, 256:512], in_=lb[:, 0:256], func=ACTF.Copy, scale=hn[:, j, 0:1])
             t8s[n] = t
 
         def stage8_sums(n):
@@ -258,20 +260,26 @@ def tile_butterflylayer_kernel(tc, x, w_in, w_out, b_out, a_pad, b_pad, out):
         def second(m):
             bt, oc = m // 4, m % 4
             gq, gs = gqs[bt]
-            acc = accp.tile([P, 512], F32, name="acc2", tag="acc")
-            for c in range(4):
-                wq, ws = wcodes[8 + 2 * oc + c // 2]
-                r = 512 * (c % 2)
-                nc.tensor.matmul_mx(out=acc[:], lhsT=gq[:, 128 * c:128 * c + 128].bitcast(FP8X4), lhsT_scale=gs[:, 128 * c:128 * c + 128],
-                                    rhs=wq[:, r:r + 512].bitcast(FP8X4), rhs_scale=ws[:, r:r + 512],
-                                    start=(c == 0), stop=(c == 3))
-            acc2[m] = acc
+            acc2[m] = []
+            n = 256 if m == 15 else 512
+            for z in range(512 // n):
+                acc = accp.tile([P, n], F32, name="acc2", tag="acc")
+                for c in range(4):
+                    wq, ws = wcodes[8 + 2 * oc + c // 2]
+                    r = 512 * (c % 2) + n * z
+                    nc.tensor.matmul_mx(out=acc[:], lhsT=gq[:, 128 * c:128 * c + 128].bitcast(FP8X4), lhsT_scale=gs[:, 128 * c:128 * c + 128],
+                                        rhs=wq[:, r:r + n].bitcast(FP8X4), rhs_scale=ws[:, r:r + n],
+                                        start=(c == 0), stop=(c == 3))
+                acc2[m].append(acc)
 
         def leave(m):
             bt, oc = m // 4, m % 4
-            osb = osp.tile([P, 512], F32, name="osb", tag="osb", align_bytes=64)
-            nc.vector.tensor_tensor(out=osb[:], in0=acc2[m][:], in1=bias[:, 512 * oc:512 * oc + 512], op=ALU.add)
-            nc.sync.dma_start(out=out[128 * bt:128 * bt + 128, 512 * oc:512 * oc + 512], in_=osb[:])
+            n = 512 // len(acc2[m])
+            for z, acc in enumerate(acc2[m]):
+                osb = osp.tile([P, n], F32, name="osb", tag="osb", align_bytes=64)
+                o = 512 * oc + n * z
+                nc.vector.tensor_tensor(out=osb[:], in0=acc[:], in1=bias[:, o:o + n], op=ALU.add)
+                nc.sync.dma_start(out=out[128 * bt:128 * bt + 128, o:o + n], in_=osb[:])
 
         identB = const.tile([P, P], BF16, name="identB")
         nc.vector.tensor_copy(out=identB[:], in_=identF[:])
@@ -303,7 +311,7 @@ def tile_butterflylayer_kernel(tc, x, w_in, w_out, b_out, a_pad, b_pad, out):
         nc.vector.tensor_copy(out=c0[:, 0:16], in_=v0ps[:, 0:16])
         nc.vector.tensor_scalar_mul(out=c0[:, 16:24], in0=v0ps[:, 8:16], scalar1=-1.0)
         hc = const.tile([P, 4, 6], F32, name="hc")
-        hn = const.tile([P, 4], F32, name="hn")
+        hn = const.tile([P, 4, 3], F32, name="hn")
 
         grp = turn_w(1, both)
         quantise_w(1, grp)
@@ -318,12 +326,14 @@ def tile_butterflylayer_kernel(tc, x, w_in, w_out, b_out, a_pad, b_pad, out):
             nc.vector.tensor_copy(out=R[:, 1, :, 0], in_=ups[:, 56:112])
             nc.vector.tensor_copy(out=R[:, 1, :, 1], in_=ups[:, 0:56])
 
-        def tables_2():
+        def tables_3():
             hps = accp.tile([P, 4, 6], F32, name="hps", tag="acc")
             for j in range(4):
                 nc.tensor.matmul(out=hps[:, j, :], lhsT=V1[:, j:j + 1].to_broadcast([P, P]), rhs=identB[:, 0:6], start=True, stop=True)
             nc.vector.tensor_copy(out=hc[:], in_=hps[:])
-            nc.vector.tensor_scalar_mul(out=hn[:], in0=hc[:, :, 3], scalar1=-1.0)
+            nc.vector.tensor_scalar_mul(out=hn[:], in0=hc[:, :, 3:6], scalar1=-1.0)
+
+        def tables_2():
             fps = accp.tile([P, 112], F32, name="fps", tag="acc")
             for z in range(2):
                 nc.tensor.matmul(out=fps[:], lhsT=E[:, z, :], rhs=R[:, z].rearrange("p r o -> p (r o)"),
@@ -358,8 +368,10 @@ def tile_butterflylayer_kernel(tc, x, w_in, w_out, b_out, a_pad, b_pad, out):
         for h in range(2, 8):
             put(at[0, h - 2], "turn", h)
         T0 = 15
+        early = [8, 9]
+        turn_at = early + [T0 + (u * 6) // 4 for u in range(8 - len(early))]
         for u in range(8):
-            put(T0 + (u * 5) // 4, "turn", 8 + u)
+            put(turn_at[u], "turn", 8 + u)
         put(6, "turnx", 1)
         ready = {}
         for half in range(2):
@@ -370,23 +382,23 @@ def tile_butterflylayer_kernel(tc, x, w_in, w_out, b_out, a_pad, b_pad, out):
                     put(k, "middle", n)
                     put(k + 1, "eight", n)
                     if j % 2 == 1:
-                        put(k + (2, 2)[half], "nine", 4 * half + 2 * (j // 2) + bt)
+                        put(k + (2, 3)[half], "nine", 4 * half + 2 * (j // 2) + bt)
                     if j == 3:
-                        k = k + (4, 4)[half] + bt * (0, 1)[half]
+                        k = k + (4, 4)[half] + bt * (0, 2)[half]
                         put(k, "ten", (2 * half + bt, 0))
                         k = k + (2, 1)[half]
                         put(k, "ten", (2 * half + bt, 1))
                         ready[2 * half + bt] = k
         for oc in range(4):
             for bt in range(4):
-                put(max(T0 + ((2 * oc + 1) * 5) // 4 + 2, ready[bt] + 1), "second", 4 * bt + oc)
+                put(max(turn_at[2 * oc + 1] + 2, ready[bt] + 1), "second", 4 * bt + oc)
         last_step = max(k for k, kind in steps)
         left = []
         last = []
         for k in range(last_step + 1):
             late = k >= 99
-            pq = (1, 4)[late]
-            pl = (0, 4)[late]
+            pq = (1, 2)[late]
+            pl = (4, 3)[late]
             pp = (0, 1)[late]
 
             def vec(pos):
@@ -397,6 +409,8 @@ def tile_butterflylayer_kernel(tc, x, w_in, w_out, b_out, a_pad, b_pad, out):
                     for m in left:
                         leave(m)
 
+            if k == 1:
+                LT = tables_2()
             for n in steps.get((k, "eight"), []):
                 stage8_products(n)
             vec(0)
@@ -425,19 +439,20 @@ def tile_butterflylayer_kernel(tc, x, w_in, w_out, b_out, a_pad, b_pad, out):
                         quantise_g(bt)
                 vec(3)
             turned = []
+            if k < 1:
+                first(rows[k])
+                stage0_products(rows[k])
             if k == 0:
-                first(rows[0])
+                tables_1()
             for u in steps.get((k, "turn"), []):
-                turned.append((u, turn_w(u, (sc, sc, sc, sc) if k < 0 or k >= 0 else (sc, sc, sc, vc))))
+                turned.append((u, turn_w(u, (sc, sc, sc, vc) if u in [8, 9] else (sc, sc, sc, sc))))
             grpx = None
             if (k, "turnx") in steps:
                 grpx = turn_x(1, (sc, sc, sc, sc))
-            if k == 1:
-                LT = tables_2()
+            if k == 2:
+                tables_3()
             if 1 <= k < 16:
                 first(rows[k])
-            if k == 0:
-                tables_1()
             for n in steps.get((k, "middle"), []):
                 middle(n)
             if not (late and True):
@@ -449,7 +464,7 @@ def tile_butterflylayer_kernel(tc, x, w_in, w_out, b_out, a_pad, b_pad, out):
                 for n in steps.get((k, "nine"), []):
                     stage9_sums(n)
                 vec(3)
-            if k < 16:
+            if 1 <= k < 16:
                 stage0_products(rows[k])
             if not (late and True):
                 for bt, c in steps.get((k, "ten"), []):

@@ -42,6 +42,8 @@ def tile_butterflylayer_kernel(tc, x, w_in, w_out, b_out, a_pad, b_pad, out):
         nc.scalar.activation(out=spark[:], in_=spark[:], func=ACTF.Copy, scale=1.0)
         identF = const.tile([P, P], F32, name="identF")
         make_identity(nc, identF[:])
+        cold = const.tile([P, 512], BF16, name="cold")
+        nc.vector.memset(cold[:], 0.0)
         V0 = const.tile([P, P], BF16, name="V0")
         nc.vector.memset(V0[:], 0.0)
         U = const.tile([P, P], BF16, name="U")
@@ -295,10 +297,18 @@ def tile_butterflylayer_kernel(tc, x, w_in, w_out, b_out, a_pad, b_pad, out):
                                         in_=identF[:].rearrange("p (q z r) -> p q z r", z=2, r=1 << i), axis=AXIS.X, op=ALU.add)
 
         both = (vc, sc, vc, sc)
+        def warm(n):
+            wb = accp.tile([P, 512], F32, name="wb", tag="acc")
+            for i in range(n):
+                nc.tensor.matmul(out=wb[:], lhsT=cold[:, 0:P], rhs=cold[:], start=True, stop=True)
+
+        warm(4)
         grp = turn_x(0, both)
         quantise_x(0, grp)
+        warm(3)
         grp = turn_w(0, both)
         quantise_w(0, grp)
+        warm(2)
 
         eps = accp.tile([P, 2, P], F32, name="eps", tag="acc")
         for z in range(2):

@@ -29,7 +29,7 @@ def tile_butterflylayer_kernel(tc, x, w_in, w_out, b_out, a_pad, b_pad, out):
         k4 = ctx.enter_context(tc.tile_pool(name="k4", bufs=3))
         ggp = ctx.enter_context(tc.tile_pool(name="ggp", bufs=2))
         gqp = ctx.enter_context(tc.tile_pool(name="gqp", bufs=4))
-        osp = ctx.enter_context(tc.tile_pool(name="osp", bufs=5))
+        osp = ctx.enter_context(tc.tile_pool(name="osp", bufs=6))
         tps = ctx.enter_context(tc.psum_pool(name="tps", bufs=4))
         accp = ctx.enter_context(tc.psum_pool(name="accp", bufs=4))
         ctx.enter_context(tc.manual_schedule())
@@ -74,7 +74,7 @@ def tile_butterflylayer_kernel(tc, x, w_in, w_out, b_out, a_pad, b_pad, out):
             nc.sync.dma_start(out=raw[:].rearrange("p (t k) -> p t k", t=4),
                               in_=w_out[512 * oc:512 * oc + 512, 1024 * cp:1024 * cp + 1024].rearrange("(t p) k -> p t k", p=P))
 
-        XB = 6
+        XB = 7
         load_x(0)
         load_in(0)
 
@@ -104,9 +104,10 @@ def tile_butterflylayer_kernel(tc, x, w_in, w_out, b_out, a_pad, b_pad, out):
             if h == XB:
                 load_x(1)
         bias = const.tile([P, 2048], BF16, name="bias")
-        nc.sync.dma_start(out=bias[:], in_=b_out.partition_broadcast(P))
         for un in range(8):
             load_out(un)
+            if un == 1:
+                nc.sync.dma_start(out=bias[:], in_=b_out.partition_broadcast(P))
 
         def turn(raw, kind, copies):
             rawW = raw[:].bitcast(F32)
@@ -377,9 +378,7 @@ def tile_butterflylayer_kernel(tc, x, w_in, w_out, b_out, a_pad, b_pad, out):
 
         for h in range(2, 8):
             put(at[0, h - 2], "turn", h)
-        T0 = 15
-        early = [8, 9]
-        turn_at = early + [T0 + (u * 6) // 4 for u in range(8 - len(early))]
+        turn_at = [8, 9, 15, 16, 18, 19, 21, 22]
         for u in range(8):
             put(turn_at[u], "turn", 8 + u)
         put(6, "turnx", 1)

from contextlib import ExitStack

import concourse.mybir as mybir
from concourse.masks import make_identity

F32 = mybir.dt.float32
BF16 = mybir.dt.bfloat16
U32 = mybir.dt.uint32
U8 = mybir.dt.uint8
FP8X4 = mybir.dt.float8_e4m3fn_x4
ALU = mybir.AluOpType
ACTF = mybir.ActivationFunctionType
AXIS = mybir.AxisListType
P = 128
HALF = 256
FLOPS = 2 * 2 * 512 * 2048 * 2048 + 11 * 3 * 512 * 2048


def tile_butterflylayer_kernel(tc, x, w_in, w_out, b_out, a_pad, b_pad, out):
    nc = tc.nc
    pads = (a_pad, b_pad)
    with ExitStack() as ctx:
        const = ctx.enter_context(tc.tile_pool(name="const", bufs=1))
        rawp = ctx.enter_context(tc.tile_pool(name="rawp", bufs=6))
        grpp = ctx.enter_context(tc.tile_pool(name="grpp", bufs=3))
        wqp = ctx.enter_context(tc.tile_pool(name="wqp", bufs=10))
        k2 = ctx.enter_context(tc.tile_pool(name="k2", bufs=4))
        s0p = ctx.enter_context(tc.tile_pool(name="s0p", bufs=5))
        k4 = ctx.enter_context(tc.tile_pool(name="k4", bufs=3))
        ggp = ctx.enter_context(tc.tile_pool(name="ggp", bufs=2))
        gqp = ctx.enter_context(tc.tile_pool(name="gqp", bufs=4))
        osp = ctx.enter_context(tc.tile_pool(name="osp", bufs=6))
        tps = ctx.enter_context(tc.psum_pool(name="tps", bufs=4))
        accp = ctx.enter_context(tc.psum_pool(name="accp", bufs=4))
        ctx.enter_context(tc.manual_schedule())

        sc = nc.scalar.copy
        vc = nc.vector.tensor_copy

        spark = const.tile([P, 1], F32, name="spark")
        nc.vector.memset(spark[:], 0.0)
        nc.scalar.activation(out=spark[:], in_=spark[:], func=ACTF.Copy, scale=1.0)
        identF = const.tile([P, P], F32, name="identF")
        make_identity(nc, identF[:])
        cold = const.tile([P, 512], BF16, name="cold")
        nc.vector.memset(cold[:], 0.0)
        V0 = const.tile([P, P], BF16, name="V0")
        nc.vector.memset(V0[:], 0.0)
        U = const.tile([P, P], BF16, name="U")
        nc.vector.memset(U[:], 0.0)
        V1 = const.tile([P, 4], BF16, name="V1")
        nc.vector.memset(V1[:], 0.0)

        raws = {}

        def new_raw(key):
            raw = rawp.tile([P, 4096], BF16, name="raw", tag="raw")
            raws[key] = raw
            return raw

        def load_x(half):
            raw = new_raw(("x", half))
            for a in range(2):
                nc.sync.dma_start(out=raw[:].rearrange("p (t k) -> p t k", t=2)[:, :, 1024 * a:1024 * a + 1024],
                                  in_=x[HALF * half:HALF * half + HALF, 1024 * a:1024 * a + 1024].rearrange("(t p) k -> p t k", p=P))

        def load_in(h):
            raw = new_raw(h)
            nc.sync.dma_start(out=raw[:], in_=w_in[256 * h:256 * h + 256, :].rearrange("(p e) k -> p (e k)", e=2))

        def load_out(un):
            oc, cp = un // 2, un % 2
            raw = new_raw(8 + un)
            nc.sync.dma_start(out=raw[:].rearrange("p (t k) -> p t k", t=4),
                              in_=w_out[512 * oc:512 * oc + 512, 1024 * cp:1024 * cp + 1024].rearrange("(t p) k -> p t k", p=P))

        XB = 7
        load_x(0)
        load_in(0)

        def load_table(queue, i):
            n = 64 >> i
            off = P - 2 * n
            for arr in range(2):
                r0 = 56 * arr + 8 * i
                queue.dma_start(out=U[r0:r0 + 8, off:off + n],
                                in_=pads[arr][i + 1:i + 2, 0:8 * n].rearrange("o (h q) -> (o h) q", q=n))

        ctx.enter_context(nc.allow_non_contiguous_dma(reason="small coefficient tables"))
        for arr in range(2):
            nc.gpsimd.dma_start(out=V0[8 * arr:8 * arr + 8, :],
                                in_=pads[arr][0:1, :].rearrange("o (h c) -> (o h) c", c=P))
        for i in range(3):
            load_table(nc.scalar, i)
        for i in range(5, 7):
            load_table(nc.gpsimd, i)
        for arr in range(2):
            nc.gpsimd.dma_start(out=V1[3 * arr:3 * arr + 3, :], in_=pads[arr][8:11, 0:4])
        for h in range(1, 8):
            load_in(h)
            if h == 2:
                for i in range(3, 5):
                    load_table(nc.sync, i)
            if h == XB:
                load_x(1)
        bias = const.tile([P, 2048], BF16, name="bias")
        for un in range(8):
            load_out(un)
            if un == 1:
                nc.sync.dma_start(out=bias[:], in_=b_out.partition_broadcast(P))

        def turn(raw, kind, copies):
            rawW = raw[:].bitcast(F32)
            grp = grpp.tile([P, 4096], BF16, name="grp", tag="grp", align_bytes=64)
            grpW = grp[:].bitcast(F32)
            for b in range(4):
                bank = tps.tile([P, 512], F32, name="bank", tag="tp")
                for u in range(2):
                    for s in range(2):
                        if kind == "out":
                            src = (2 * (b % 2) + s) * 512 + 256 * (b // 2) + 128 * u
                        elif kind == "in":
                            src = (b // 2) * 1024 + 256 * (2 * (b % 2) + s) + 128 * u
                        else:
                            src = s * 1024 + 256 * b + 128 * u
                        d = u * 256 + s * 128
                        nc.tensor.transpose(bank[:, d:d + 128], rawW[:, src:src + 128], identF[:])
                copies[b](out=grpW[:, 512 * b:512 * b + 512].rearrange("p (c u) -> p c u", u=2),
                          in_=bank[:].rearrange("p (u c) -> p c u", u=2))
            return grp

        def quantise(grp, codes, scales):
            nc.vector.quantize_mx(out=codes.bitcast(FP8X4), scales=scales, in_=grp[:])

        xq = [const.tile([P, 1024], U32, name="xq%d" % half, align_bytes=64) for half in range(2)]
        xs = [const.tile([P, 1024], U8, name="xs%d" % half, align_bytes=64) for half in range(2)]
        wcodes = {}

        def turn_x(half, copies):
            return turn(raws["x", half], "x", copies)

        def quantise_x(half, grp):
            quantise(grp, xq[half][:], xs[half][:])

        def turn_w(k, copies):
            return turn(raws[k], "in" if k < 8 else "out", copies)

        def quantise_w(k, grp):
            wq = wqp.tile([P, 1024], U32, name="wq", tag="wq", align_bytes=64)
            ws = wqp.tile([P, 1024], U8, name="ws", tag="ws", align_bytes=64)
            quantise(grp, wq[:], ws[:])
            wcodes[k] = (wq, ws)

        accs = {}
        t0s = {}
        s0s = {}

        def first(row):
            half, h = row
            wq, ws = wcodes[h]
            acc = accp.tile([P, 512], F32, name="acc", tag="acc")
            for e in range(2):
                for g in range(4):
                    c = (4 * e + g) * 128
                    m = HALF * g
                    nc.tensor.matmul_mx(out=acc[:, HALF * e:HALF * e + HALF], lhsT=wq[:, c:c + 128].bitcast(FP8X4), lhsT_scale=ws[:, c:c + 128],
                                        rhs=xq[half][:, m:m + HALF].bitcast(FP8X4), rhs_scale=xs[half][:, m:m + HALF],
                                        start=(g == 0), stop=(g == 3))
            accs[row] = acc

        def stage0_products(row):
            h = row[1]
            acc = accs[row]
            t = k2.tile([P, 512], F32, name="t0", tag="t", align_bytes=64)
            nc.scalar.activation(out=t[:, 0:HALF], in_=acc[:, HALF:512], func=ACTF.Copy, scale=c0[:, 8 + h:9 + h])
            nc.scalar.activation(out=t[:, HALF:512], in_=acc[:, 0:HALF], func=ACTF.Copy, scale=c0[:, 16 + h:17 + h])
            t0s[row] = t

        def stage0_sums(row):
            h = row[1]
            s0 = s0p.tile([P, 512], F32, name="s0", tag="s0", align_bytes=64)
            nc.vector.scalar_tensor_tensor(out=s0[:], in0=accs[row][:], scalar=c0[:, h:h + 1], in1=t0s[row][:], op0=ALU.mult, op1=ALU.add)
            s0s[row] = s0

        ys = [const.tile([P, 4, 1024], F32, name="y%d" % half, align_bytes=64) for half in range(2)]
        lbs = {}
        t8s = {}
        done8 = set()
        done9 = set()

        def middle(n):
            half, j, bt = n // 8, (n // 2) % 4, n % 2
            lb = accp.tile([P, 512], F32, name="lb", tag="acc")
            for hl in range(2):
                h = 2 * j + hl
                nc.tensor.matmul(out=lb[:, 256 * hl:256 * hl + 256], lhsT=LT[:, h, :],
                                 rhs=s0s[half, h][:].rearrange("p (e t b) -> p e t b", e=2, t=2)[:, :, bt, :], start=True, stop=True)
            lbs[n] = lb

        def stage8_products(n):
            j = (n // 2) % 4
            lb = lbs[n]
            t = k2.tile([P, 512], F32, name="t8", tag="t", align_bytes=64)
            nc.scalar.activation(out=t[:, 0:256], in_=lb[:, 256:512], func=ACTF.Copy, scale=hc[:, j, 3:4])
            nc.scalar.activation(out=t[:, 256:512], in_=lb[:, 0:256], func=ACTF.Copy, scale=hn[:, j, 0:1])
            t8s[n] = t

        def stage8_sums(n):
            half, j, bt = n // 8, (n // 2) % 4, n % 2
            done8.add(n)
            nc.vector.scalar_tensor_tensor(out=ys[half][:, j, 512 * bt:512 * bt + 512].rearrange("p (b t) -> p b t", t=4),
                                           in0=lbs[n][:].rearrange("p (t b) -> p b t", t=4), scalar=hc[:, j, 0:1],
                                           in1=t8s[n][:].rearrange("p (t b) -> p b t", t=4), op0=ALU.mult, op1=ALU.add)

        t9s = {}

        def stage9_products(n):
            half, j2, bt = n // 4, (n // 2) % 2, n % 2
            assert 8 * half + 4 * j2 + bt in done8 and 8 * half + 4 * j2 + 2 + bt in done8
            t = k4.tile([P, 2, 512], F32, name="t9", tag="t4k", align_bytes=64)
            nc.scalar.activation(out=t[:], in_=ys[half][:, 2 * j2:2 * j2 + 2, 512 * bt:512 * bt + 512], func=ACTF.Copy, scale=hc[:, j2, 4:5])
            t9s[n] = t

        def stage9_sums(n):
            half, j2, bt = n // 4, (n // 2) % 2, n % 2
            done9.add(n)
            cols = slice(512 * bt, 512 * bt + 512)
            y = ys[half]
            t = t9s[n]
            x0 = y[:, 2 * j2, cols]
            x1 = y[:, 2 * j2 + 1, cols]
            nc.vector.scalar_tensor_tensor(out=x0, in0=x0, scalar=hc[:, j2, 1:2], in1=t[:, 1, :], op0=ALU.mult, op1=ALU.add)
            nc.vector.scalar_tensor_tensor(out=x1, in0=x1, scalar=hc[:, j2, 1:2], in1=t[:, 0, :], op0=ALU.mult, op1=ALU.subtract)

        ggs = {}
        t10s = {}
        gqs = {}

        def stage10_products(bt, c):
            assert 4 * (bt // 2) + bt % 2 in done9 and 4 * (bt // 2) + 2 + bt % 2 in done9
            t = k4.tile([P, 2, 512], F32, name="t10", tag="t4k", align_bytes=64)
            nc.scalar.activation(out=t[:], in_=ys[bt // 2][:, c::2, 512 * (bt % 2):512 * (bt % 2) + 512], func=ACTF.Copy, scale=hc[:, 0, 5:6])
            t10s[bt, c] = t

        def stage10_sums(bt, c):
            if c == 0:
                ggs[bt] = ggp.tile([P, 4, 512], BF16, name="gg", tag="gg", align_bytes=64)
            gg = ggs[bt]
            t = t10s[bt, c]
            cols = slice(512 * (bt % 2), 512 * (bt % 2) + 512)
            y = ys[bt // 2]
            nc.vector.scalar_tensor_tensor(out=gg[:, c, :], in0=y[:, c, cols], scalar=hc[:, 0, 2:3], in1=t[:, 1, :], op0=ALU.mult, op1=ALU.add)
            nc.vector.scalar_tensor_tensor(out=gg[:, c + 2, :], in0=y[:, c + 2, cols], scalar=hc[:, 0, 2:3], in1=t[:, 0, :], op0=ALU.mult, op1=ALU.subtract)

        def quantise_g(bt):
            gq = gqp.tile([P, 512], U32, name="gq", tag="gq", align_bytes=64)
            gs = gqp.tile([P, 512], U8, name="gs", tag="gs", align_bytes=64)
            nc.vector.quantize_mx(out=gq[:].bitcast(FP8X4), scales=gs[:], in_=ggs[bt][:].rearrange("p c n -> p (c n)"))
            gqs[bt] = (gq, gs)

        acc2 = {}

        def second(m):
            bt, oc = m // 4, m % 4
            gq, gs = gqs[bt]
            acc2[m] = []
            n = 256 if m == 15 else 512
            for z in range(512 // n):
                acc = accp.tile([P, n], F32, name="acc2", tag="acc")
                for c in range(4):
                    wq, ws = wcodes[8 + 2 * oc + c // 2]
                    r = 512 * (c % 2) + n * z
                    nc.tensor.matmul_mx(out=acc[:], lhsT=gq[:, 128 * c:128 * c + 128].bitcast(FP8X4), lhsT_scale=gs[:, 128 * c:128 * c + 128],
                                        rhs=wq[:, r:r + n].bitcast(FP8X4), rhs_scale=ws[:, r:r + n],
                                        start=(c == 0), stop=(c == 3))
                acc2[m].append(acc)

        def leave(m):
            bt, oc = m // 4, m % 4
            n = 512 // len(acc2[m])
            for z, acc in enumerate(acc2[m]):
                osb = osp.tile([P, n], F32, name="osb", tag="osb", align_bytes=64)
                o = 512 * oc + n * z
                nc.vector.tensor_tensor(out=osb[:], in0=acc[:], in1=bias[:, o:o + n], op=ALU.add)
                nc.sync.dma_start(out=out[128 * bt:128 * bt + 128, o:o + n], in_=osb[:])

        identB = const.tile([P, P], BF16, name="identB")
        nc.vector.tensor_copy(out=identB[:], in_=identF[:])
        ET = const.tile([P, 2, P], F32, name="ET")
        nc.vector.memset(ET[:], 0.0)
        for i in range(7):
            n = 64 >> i
            off = P - 2 * n
            if i == 0:
                nc.vector.tensor_copy(out=ET[:, :, off:off + n].rearrange("p z q -> p q z"), in_=identF[:].rearrange("p (q z) -> p q z", z=2))
            else:
                nc.vector.tensor_reduce(out=ET[:, :, off:off + n].rearrange("p z q -> p q z"),
                                        in_=identF[:].rearrange("p (q z r) -> p q z r", z=2, r=1 << i), axis=AXIS.X, op=ALU.add)

        both = (vc, sc, vc, sc)
        def warm(n):
            wb = accp.tile([P, 512], F32, name="wb", tag="acc")
            for i in range(n):
                nc.tensor.matmul(out=wb[:], lhsT=cold[:, 0:P], rhs=cold[:], start=True, stop=True)

        warm(4)
        grp = turn_x(0, both)
        quantise_x(0, grp)
        warm(3)
        grp = turn_w(0, both)
        quantise_w(0, grp)
        warm(2)

        eps = accp.tile([P, 2, P], F32, name="eps", tag="acc")
        for z in range(2):
            nc.tensor.transpose(eps[:, z, :], ET[:, z, :], identF[:])
        v0ps = accp.tile([P, P], BF16, name="v0ps", tag="acc")
        nc.tensor.transpose(v0ps[:], V0[:], identB[:])
        E = const.tile([P, 2, P], BF16, name="E")
        nc.vector.tensor_copy(out=E[:], in_=eps[:])
        c0 = const.tile([P, 24], F32, name="c0")
        nc.vector.tensor_copy(out=c0[:, 0:16], in_=v0ps[:, 0:16])
        nc.vector.tensor_scalar_mul(out=c0[:, 16:24], in0=v0ps[:, 8:16], scalar1=-1.0)
        hc = const.tile([P, 4, 6], F32, name="hc")
        hn = const.tile([P, 4, 3], F32, name="hn")

        grp = turn_w(1, both)
        quantise_w(1, grp)
        R = const.tile([P, 2, 56, 2], BF16, name="R")
        F = const.tile([P, 7, 8, 2], F32, name="F")

        def tables_1():
            ups = accp.tile([P, P], BF16, name="ups", tag="acc")
            nc.tensor.transpose(ups[:], U[:], identB[:])
            nc.vector.tensor_copy(out=R[:, 0, :, 0], in_=ups[:, 0:56])
            nc.vector.tensor_scalar_mul(out=R[:, 0, :, 1], in0=ups[:, 56:112], scalar1=-1.0)
            nc.vector.tensor_copy(out=R[:, 1, :, 0], in_=ups[:, 56:112])
            nc.vector.tensor_copy(out=R[:, 1, :, 1], in_=ups[:, 0:56])

        def tables_3():
            hps = accp.tile([P, 4, 6], F32, name="hps", tag="acc")
            for j in range(4):
                nc.tensor.matmul(out=hps[:, j, :], lhsT=V1[:, j:j + 1].to_broadcast([P, P]), rhs=identB[:, 0:6], start=True, stop=True)
            nc.vector.tensor_copy(out=hc[:], in_=hps[:])
            nc.vector.tensor_scalar_mul(out=hn[:], in0=hc[:, :, 3:6], scalar1=-1.0)

        def tables_2():
            fps = accp.tile([P, 112], F32, name="fps", tag="acc")
            for z in range(2):
                nc.tensor.matmul(out=fps[:], lhsT=E[:, z, :], rhs=R[:, z].rearrange("p r o -> p (r o)"),
                                 start=(z == 0), stop=(z == 1))
            nc.vector.tensor_copy(out=F[:].rearrange("p i h o -> p (i h o)"), in_=fps[:])

            def outer(name, high, low, n, r):
                pair = const.tile([P, 8, n * r], F32, name=name)
                nc.vector.tensor_tensor(out=pair[:].rearrange("p h (o r) -> p h o r", o=n),
                                        in0=high.unsqueeze(3).to_broadcast([P, 8, n, r]),
                                        in1=low.unsqueeze(2).to_broadcast([P, 8, n, r]), op=ALU.mult)
                return pair[:]

            f10 = outer("f10", F[:, 1], F[:, 0], 2, 2)
            f54 = outer("f54", F[:, 5], F[:, 4], 2, 2)
            f32 = outer("f32", F[:, 3], F[:, 2], 2, 2)
            f654 = outer("f654", F[:, 6], f54, 2, 4)
            f3210 = outer("f3210", f32, f10, 4, 4)
            return outer("lt", f654, f3210, 8, 16)


        rows = [(half, h) for half in range(2) for h in range(8)]
        at = {}
        for k, row in enumerate(rows):
            at[row] = k
        steps = {}
        done = set()

        def put(k, kind, args):
            steps.setdefault((k, kind), []).append(args)

        for h in range(2, 8):
            put(at[0, h - 2], "turn", h)
        turn_at = [8, 9, 15, 16, 18, 19, 21, 22]
        for u in range(8):
            put(turn_at[u], "turn", 8 + u)
        put(6, "turnx", 1)
        ready = {}
        for half in range(2):
            for j in range(4):
                for bt in range(2):
                    k = at[half, 2 * j + 1] + 1 + bt
                    n = 8 * half + 2 * j + bt
                    put(k, "middle", n)
                    put(k + 1, "eight", n)
                    if j % 2 == 1:
                        put(k + (2, 3)[half], "nine", 4 * half + 2 * (j // 2) + bt)
                    if j == 3:
                        k = k + (4, 4)[half] + bt * (0, 2)[half]
                        put(k, "ten", (2 * half + bt, 0))
                        k = k + (2, 1)[half]
                        put(k, "ten", (2 * half + bt, 1))
                        ready[2 * half + bt] = k
        for oc in range(4):
            for bt in range(4):
                put(max(turn_at[2 * oc + 1] + 2, ready[bt] + 1), "second", 4 * bt + oc)
        last_step = max(k for k, kind in steps)
        left = []
        last = []
        for k in range(last_step + 1):
            late = k >= 99
            pq = (1, 2)[late]
            pl = (4, 3)[late]
            pp = (0, 1)[late]

            def vec(pos):
                if pos == pq:
                    for u, grp in last:
                        quantise_w(u, grp)
                if pos == pl:
                    for m in left:
                        leave(m)

            if k == 1:
                LT = tables_2()
            for n in steps.get((k, "eight"), []):
                stage8_products(n)
            vec(0)
            if 1 <= k <= 16:
                stage0_sums(rows[k - 1])
            vec(1)
            if pp == 0:
                for n in steps.get((k, "nine"), []):
                    stage9_products(n)
                for bt, c in steps.get((k, "ten"), []):
                    stage10_products(bt, c)
            for n in steps.get((k, "eight"), []):
                stage8_sums(n)
            vec(2)
            if late and True:
                if pp == 1:
                    for n in steps.get((k, "nine"), []):
                        stage9_products(n)
                    for bt, c in steps.get((k, "ten"), []):
                        stage10_products(bt, c)
                for n in steps.get((k, "nine"), []):
                    stage9_sums(n)
                for bt, c in steps.get((k, "ten"), []):
                    stage10_sums(bt, c)
                    if c == 1:
                        quantise_g(bt)
                vec(3)
            turned = []
            if k < 1:
                first(rows[k])
                stage0_products(rows[k])
            if k == 0:
                tables_1()
            for u in steps.get((k, "turn"), []):
                turned.append((u, turn_w(u, (sc, sc, sc, vc) if u in [8, 9] else (sc, sc, sc, sc))))
            grpx = None
            if (k, "turnx") in steps:
                grpx = turn_x(1, (sc, sc, sc, sc))
            if k == 2:
                tables_3()
            if 1 <= k < 16:
                first(rows[k])
            for n in steps.get((k, "middle"), []):
                middle(n)
            if not (late and True):
                if pp == 1:
                    for n in steps.get((k, "nine"), []):
                        stage9_products(n)
                    for bt, c in steps.get((k, "ten"), []):
                        stage10_products(bt, c)
                for n in steps.get((k, "nine"), []):
                    stage9_sums(n)
                vec(3)
            if 1 <= k < 16:
                stage0_products(rows[k])
            if not (late and True):
                for bt, c in steps.get((k, "ten"), []):
                    stage10_sums(bt, c)
                    if c == 1 and False:
                        quantise_g(bt)
            vec(4)
            if not (late and True) and not False:
                for bt, c in steps.get((k, "ten"), []):
                    if c == 1:
                        quantise_g(bt)
            left = steps.get((k, "second"), [])
            last = turned
            for m in left:
                second(m)
            if grpx is not None:
                quantise_x(1, grpx)
        for m in left:
            leave(m)
